import numpy as np
import ml_dtypes


def mxq(x, axis, fmt="e4m3"):
    dtype, down = {"e4m3": (ml_dtypes.float8_e4m3fn, 7), "e5m2": (ml_dtypes.float8_e5m2, 14)}[fmt]
    v = np.moveaxis(np.asarray(x, np.float32).astype(ml_dtypes.bfloat16).astype(np.float64), axis, -1)
    blocks = v.reshape(v.shape[:-1] + (-1, 32))
    amax = np.abs(blocks).max(-1, keepdims=True)
    byte = np.maximum(np.where(amax > 0, np.frexp(amax)[1] - 1 + 127, 0) - down, 1)
    scale = np.exp2(byte - 127.0)
    codes = (blocks / scale).astype(np.float32).astype(dtype).astype(np.float64)
    return np.moveaxis((codes * scale).reshape(v.shape), -1, axis)


WIDE = False


def mx_kscale(k):
    if not WIDE:
        return np.ones(k)
    levels = np.array([10, -10, 5, -5, 0])
    a = np.random.permutation(np.resize(levels, k // 512 * 4)).reshape(k // 512, 4)
    idx = np.arange(k)
    return np.exp2(a[idx // 512, idx % 128 // 32])


BF16 = ml_dtypes.bfloat16


def bf(x):
    return np.asarray(x, np.float32).astype(BF16)


def f64(x):
    return np.asarray(x).astype(np.float64)


B, D, H = 4096, 1024, 256
QH = H % 2**9 == 0


def sigmoid(v):
    return 1.0 / (1.0 + np.exp(-v))


def xavier(rows, cols):
    limit = np.sqrt(6.0 / (rows + cols))
    return np.random.uniform(-limit, limit, (rows, cols))


def setup_inputs():
    s = mx_kscale(D)
    t = mx_kscale(H) if QH else np.ones(H)
    inp = {"x": bf(np.random.standard_normal((B, D)) * s), "h0": bf(np.random.standard_normal((B, H)) * t), "c0": bf(np.random.standard_normal((B, H)))}
    for n in ("i", "f", "g", "o"):
        inp["W_i" + n] = bf(xavier(H, D) / s)
        inp["b_i" + n] = bf(np.random.standard_normal(H) * 0.1)
        inp["W_h" + n] = bf(xavier(H, H) / t)
        inp["b_h" + n] = bf(np.random.standard_normal(H) * 0.1)
    return inp


def reference(x, h0, c0,
              W_ii, b_ii, W_hi, b_hi,
              W_if, b_if, W_hf, b_hf,
              W_ig, b_ig, W_hg, b_hg,
              W_io, b_io, W_ho, b_ho):
    Wx = np.concatenate([f64(W_ii), f64(W_if), f64(W_ig), f64(W_io)], axis=0)
    Wh = np.concatenate([f64(W_hi), f64(W_hf), f64(W_hg), f64(W_ho)], axis=0)
    b = np.concatenate([f64(b_ii) + f64(b_hi), f64(b_if) + f64(b_hf), f64(b_ig) + f64(b_hg), f64(b_io) + f64(b_ho)])
    gx = mxq(f64(x), 1, "e4m3") @ mxq(Wx, 1, "e4m3").T
    if QH:
        gh = mxq(f64(h0), 1, "e4m3") @ mxq(Wh, 1, "e4m3").T
    else:
        gh = f64(h0) @ Wh.T
    gates = gx + gh + b
    i_t = sigmoid(gates[:, 0 * H:1 * H])
    f_t = sigmoid(gates[:, 1 * H:2 * H])
    g_t = np.tanh(gates[:, 2 * H:3 * H])
    o_t = sigmoid(gates[:, 3 * H:4 * H])
    c_t = f_t * c0_f(c0) + i_t * g_t
    h_t = o_t * np.tanh(c_t)
    return (h_t, c_t)


def c0_f(c0):
    return f64(c0)

@@ -1,0 +1,331 @@
+from contextlib import ExitStack
+
+import concourse.mybir as mybir
+from concourse.masks import make_identity
+
+F32 = mybir.dt.float32
+BF16 = mybir.dt.bfloat16
+U32 = mybir.dt.uint32
+U8 = mybir.dt.uint8
+FP8X4 = mybir.dt.float8_e4m3fn_x4
+AF = mybir.ActivationFunctionType
+ALU = mybir.AluOpType
+
+B, D, H = 4096, 1024, 256
+P = 128
+NT = B // P
+G4 = 4 * H
+HALF = 512
+CH = 4
+NCH = NT // CH
+FLOPS = 2 * B * (D + H) * G4
+
+PIN = True
+LEAD = 5
+XL = 2
+V_PAIRS = 3
+XBUFS = 4
+
+
+def tile_lstmcell_t_kernel(
+    tc, x, h0, c0,
+    W_ii, b_ii, W_hi, b_hi,
+    W_if, b_if, W_hf, b_hf,
+    W_ig, b_ig, W_hg, b_hg,
+    W_io, b_io, W_ho, b_ho,
+    out_0, out_1,
+):
+    nc = tc.nc
+    w_in = (W_ii, W_if, W_io, W_ig)
+    w_rec = (W_hi, W_hf, W_ho, W_hg)
+    b_in = (b_ii, b_if, b_io, b_ig)
+    b_rec = (b_hi, b_hf, b_ho, b_hg)
+    xv = x.rearrange("(p t) k -> p t k", t=NT)
+    hv = h0.rearrange("(p t) k -> p t k", t=NT)
+    cv = c0.rearrange("(p t) k -> p t k", t=NT)
+    hout = out_0.rearrange("(p t) n -> p t n", t=NT)
+    cout = out_1.rearrange("(p t) n -> p t n", t=NT)
+
+    with ExitStack() as ctx:
+        if PIN:
+            ctx.enter_context(tc.manual_schedule())
+        const = ctx.enter_context(tc.tile_pool(name="const", bufs=1))
+        xin = ctx.enter_context(tc.tile_pool(name="xin", bufs=XBUFS))
+        work = ctx.enter_context(tc.tile_pool(name="work", bufs=3))
+        psum = ctx.enter_context(tc.psum_pool(name="psum", bufs=1))
+
+        ident = const.tile([P, P], F32, name="ident")
+        ones = const.tile([P, P], BF16, name="ones")
+        brow = const.tile([P, G4], BF16, name="brow")
+        bias = const.tile([P, G4], F32, name="bias")
+        warm = const.tile([P, 2], F32, name="warm")
+        whraw = [const.tile([P, 2, H], BF16, name="whraw%d" % g) for g in range(4)]
+        whw = const.tile([P, G4], F32, name="whw")
+        wraw = [const.tile([P, 2, D], BF16, name="wraw%d" % g) for g in range(4)]
+        wgrp = const.tile([P, 2, G4, 2], F32, name="wgrp", align_bytes=64)
+        wc = const.tile([P, 2, G4], U32, name="wc", align_bytes=64)
+        ws = const.tile([P, 2, G4], U8, name="ws", align_bytes=64)
+        h0raw = const.tile([P, NT, H], BF16, name="h0raw")
+        h0w = const.tile([P, NT, P], F32, name="h0w")
+        c0sb = const.tile([P, NT, H], BF16, name="c0sb")
+
+        xch = {}
+        xts = {}
+        grps = {}
+        xcs = {}
+        xss = {}
+        ghs = {}
+        gxs = {}
+        tsbs = {}
+        acts = {}
+        cts = {}
+        tchs = {}
+
+        def load_x(c):
+            xch[c] = xin.tile([P, CH, D], BF16, name="xch%d" % c, tag="xch")
+            nc.sync.dma_start(out=xch[c][:], in_=xv[:, c * CH:(c + 1) * CH, :])
+
+        def load_h0(t0, t1):
+            nc.sync.dma_start(out=h0raw[:, t0:t1, :], in_=hv[:, t0:t1, :])
+
+        def load_c0(t0, t1):
+            nc.sync.dma_start(out=c0sb[:, t0:t1, :], in_=cv[:, t0:t1, :])
+
+        def load_bias(eng, g):
+            eng.dma_start(out=brow[0:1, g * H:(g + 1) * H], in_=b_in[g].unsqueeze(0))
+            eng.dma_start(out=brow[1:2, g * H:(g + 1) * H], in_=b_rec[g].unsqueeze(0))
+
+        def load_wh(g):
+            nc.sync.dma_start(out=whraw[g][:], in_=w_rec[g].rearrange("(j p) k -> p j k", p=P))
+
+        def load_w(g):
+            nc.sync.dma_start(out=wraw[g][:], in_=w_in[g].rearrange("(j p) k -> p j k", p=P))
+
+        def bank(tag, name):
+            return psum.tile([P, HALF], F32, name=name, tag=tag, bufs=(2 if tag == "xt" else 3))
+
+        def half(h):
+            return slice(h * HALF, (h + 1) * HALF)
+
+        def tr(dst, q, src):
+            nc.tensor.transpose(out=dst[:, q * P:(q + 1) * P], in_=src, identity=ident[:])
+
+        def pairs_view(ap):
+            return ap.bitcast(BF16).rearrange("p (n e) -> p n e", e=2)
+
+        def grouped_read(pb):
+            return pb[:].rearrange("p (g u r) -> p g r u", g=2, u=2)
+
+        make_identity(nc, ident[:])
+        nc.vector.memset(warm[:], 0.0)
+        nc.vector.memset(brow[:], 0.0)
+        nc.vector.memset(ones[:], 1.0)
+        load_bias(nc.scalar, 0)
+        load_bias(nc.scalar, 1)
+        load_wh(0)
+        load_wh(1)
+        load_h0(0, 4)
+        load_wh(2)
+        load_wh(3)
+        load_bias(nc.sync, 2)
+        load_bias(nc.sync, 3)
+        load_w(0)
+        load_w(1)
+        load_x(0)
+        load_w(2)
+        load_w(3)
+        load_h0(4, 8)
+        load_x(1)
+        load_c0(0, 8)
+        load_x(2)
+        load_h0(8, 16)
+        load_x(3)
+        load_c0(8, 16)
+        load_h0(16, 32)
+        load_c0(16, 32)
+        nc.scalar.activation(out=warm[:, 1:2], in_=warm[:, 0:1], func=AF.Sigmoid)
+
+        def wh_bank(b, tag, copy):
+            pb = bank(tag, "whp%d" % b)
+            for i in range(2):
+                for j in range(2):
+                    tr(pb, 2 * i + j, whraw[2 * b + i][:, j, :].bitcast(F32))
+            copy(out=whw[:, half(b)], in_=pb[:])
+
+        def h0_tr(c, pb):
+            return [("t", pb, j, h0raw[:, c * CH + j, :].bitcast(F32)) for j in range(CH)]
+
+        def h0_copy(c, pb, copy):
+            copy(out=h0w[:, c * CH:(c + 1) * CH, :].rearrange("p t r -> p (t r)"), in_=pb[:])
+
+        def bias_bank(h, tag, copy):
+            pb = bank(tag, "bp%d" % h)
+            nc.tensor.matmul(out=pb[:], lhsT=ones[:], rhs=brow[:, half(h)], start=True, stop=True)
+            copy(out=bias[:, half(h)], in_=pb[:])
+
+        def run(op):
+            if op[0] == "t":
+                tr(op[1], op[2], op[3])
+            else:
+                t, h, e = op[1], op[2], op[3]
+                nc.tensor.matmul(
+                    out=ghs[(t, h)][:],
+                    lhsT=pairs_view(h0w[:, t, :])[:, :, e],
+                    rhs=pairs_view(whw[:, half(h)])[:, :, e],
+                    start=(e == 0),
+                    stop=(e == 1),
+                )
+
+        def weave(mm, trs):
+            gaps = max(len(mm) - 1, 1)
+            per = (len(trs) + gaps - 1) // gaps
+            i = 0
+            for n, m in enumerate(mm):
+                run(m)
+                if n < len(mm) - 1:
+                    for op in trs[i:i + per]:
+                        run(op)
+                    i += per
+            for op in trs[i:]:
+                run(op)
+
+        wh_bank(0, "xt", nc.vector.tensor_copy)
+        pb0 = bank("xt", "h0p0")
+        weave([], h0_tr(0, pb0))
+        h0_copy(0, pb0, nc.scalar.copy)
+        bias_bank(0, "gx", nc.vector.tensor_copy)
+        wh_bank(1, "gx", nc.scalar.copy)
+        bias_bank(1, "gx", nc.vector.tensor_copy)
+
+        def w_gate(g):
+            for j in range(2):
+                pb = bank("gx", "wp%d_%d" % (g, j))
+                ww = wraw[g][:, j, :].bitcast(F32)
+                for q in range(4):
+                    tr(pb, q, ww[:, q * P:(q + 1) * P])
+                n0 = g * H + j * P
+                nc.scalar.copy(out=wgrp[:, :, n0:n0 + P, :], in_=grouped_read(pb))
+
+        def w_quant(h):
+            for g in range(2):
+                nc.vector.quantize_mx(
+                    out=wc[:, g, half(h)].bitcast(FP8X4),
+                    scales=ws[:, g, half(h)],
+                    in_=wgrp[:, g, half(h), :].rearrange("p n u -> p (n u)").bitcast(BF16),
+                )
+
+        def x_copy(t):
+            grps[t] = work.tile([P, 2, P, 2], F32, name="grp%d" % t, tag="grp", bufs=3, align_bytes=64)
+            nc.scalar.copy(out=grps[t][:], in_=grouped_read(xts[t]))
+
+        def x_quant(t):
+            xcs[t] = work.tile([P, 2 * P], U32, name="xc%d" % t, tag="xc", bufs=XL + 2, align_bytes=64)
+            xss[t] = work.tile([P, 2 * P], U8, name="xs%d" % t, tag="xs", bufs=XL + 2, align_bytes=64)
+            nc.vector.quantize_mx(
+                out=xcs[t][:].bitcast(FP8X4),
+                scales=xss[t][:],
+                in_=grps[t][:].rearrange("p g r u -> p (g r u)").bitcast(BF16),
+            )
+
+        def m_passes(t):
+            for h in range(2):
+                gxs[(t, h)] = bank("gx", "gx%d_%d" % (t, h))
+                for g in range(2):
+                    nc.tensor.matmul_mx(
+                        out=gxs[(t, h)][:],
+                        lhsT=xcs[t][:, g * P:(g + 1) * P].bitcast(FP8X4),
+                        lhsT_scale=xss[t][:, g * P:(g + 1) * P],
+                        rhs=wc[:, g, half(h)].bitcast(FP8X4),
+                        rhs_scale=ws[:, g, half(h)],
+                        start=(g == 0),
+                        stop=(g == 1),
+                    )
+
+        def a_op(t, h):
+            nc.vector.tensor_tensor(out=tsbs[t][:, half(h)], in0=ghs[(t, h)][:], in1=bias[:, half(h)], op=ALU.add)
+
+        def b_op(t, h):
+            nc.vector.tensor_tensor(out=tsbs[t][:, half(h)], in0=gxs[(t, h)][:], in1=tsbs[t][:, half(h)], op=ALU.add)
+
+        def c_op(t):
+            if t % 2 == 0:
+                acts[t // 2] = work.tile([P, 2, G4], F32, name="act%d" % (t // 2), tag="act", bufs=3)
+            a = acts[t // 2]
+            nc.scalar.activation(out=a[:, t % 2, 0:3 * H], in_=tsbs[t][:, 0:3 * H], func=AF.Sigmoid)
+            nc.scalar.activation(out=a[:, t % 2, 3 * H:G4], in_=tsbs[t][:, 3 * H:G4], func=AF.Tanh)
+
+        def d_eng(k):
+            return nc.vector if k >= NT // 2 - V_PAIRS else nc.gpsimd
+
+        def d1(k):
+            eng = d_eng(k)
+            a = acts[k]
+            p1 = work.tile([P, 2, H], F32, name="p1_%d" % k, tag="p1", bufs=2)
+            p2 = work.tile([P, 2, H], F32, name="p2_%d" % k, tag="p2", bufs=2)
+            cts[k] = work.tile([P, 2, H], F32, name="ct%d" % k, tag="ct", bufs=3)
+            eng.tensor_tensor(out=p1[:], in0=a[:, :, H:2 * H], in1=c0sb[:, 2 * k:2 * k + 2, :], op=ALU.mult)
+            eng.tensor_tensor(out=p2[:], in0=a[:, :, 0:H], in1=a[:, :, 3 * H:G4], op=ALU.mult)
+            eng.tensor_tensor(out=cts[k][:], in0=p1[:], in1=p2[:], op=ALU.add)
+            nc.sync.dma_start(out=cout[:, 2 * k:2 * k + 2, :], in_=cts[k][:])
+
+        def tanh_c(k):
+            tchs[k] = work.tile([P, 2, H], F32, name="tch%d" % k, tag="tch", bufs=2)
+            nc.scalar.activation(out=tchs[k][:], in_=cts[k][:], func=AF.Tanh)
+
+        def dh(k):
+            ht = work.tile([P, 2, H], F32, name="ht%d" % k, tag="ht", bufs=3)
+            d_eng(k).tensor_tensor(out=ht[:], in0=acts[k][:, :, 2 * H:3 * H], in1=tchs[k][:], op=ALU.mult)
+            nc.sync.dma_start(out=hout[:, 2 * k:2 * k + 2, :], in_=ht[:])
+
+        for s in range(NT + LEAD):
+            tM = s - LEAD
+            tX = tM + XL
+            tq = tX - 1
+            mm = []
+            trs = []
+            hc = None
+            if s < NT:
+                tsbs[s] = work.tile([P, G4], F32, name="tsb%d" % s, tag="tsb", bufs=LEAD + 3)
+                for h in range(2):
+                    ghs[(s, h)] = bank("gh", "gh%d_%d" % (s, h))
+                mm = [("m", s, h, e) for h in range(2) for e in range(2)]
+            if 0 <= tX < NT:
+                xts[tX] = bank("xt", "xt%d" % tX)
+                xw = xch[tX // CH][:, tX % CH, :].bitcast(F32)
+                trs = trs + [("t", xts[tX], q, xw[:, q * P:(q + 1) * P]) for q in range(4)]
+            if s % CH == 2 and s + 2 < NT:
+                hc = (s + 2) // CH
+                hpb = bank("xt", "h0p%d" % hc)
+                trs = trs + h0_tr(hc, hpb)
+            weave(mm, trs)
+            if s < 4:
+                w_gate(s)
+            if 0 <= tM:
+                m_passes(tM)
+            if 0 <= tX < NT:
+                x_copy(tX)
+                if tX % CH == CH - 1 and tX // CH + XBUFS < NCH:
+                    load_x(tX // CH + XBUFS)
+            if hc is not None:
+                h0_copy(hc, hpb, nc.scalar.copy)
+            if s < NT:
+                a_op(s, 0)
+                a_op(s, 1)
+            if s == LEAD - 2:
+                w_quant(0)
+            if s == LEAD - 1:
+                w_quant(1)
+            if 0 <= tq < NT:
+                x_quant(tq)
+            if 0 <= tM:
+                b_op(tM, 0)
+                b_op(tM, 1)
+                c_op(tM)
+                if tM % 2 == 1:
+                    k = tM // 2
+                    d1(k)
+                    if k >= 1:
+                        tanh_c(k - 1)
+                        dh(k - 1)
+        tanh_c(NT // 2 - 1)
+        dh(NT // 2 - 1)

@@ -22,8 +22,9 @@ FLOPS = 2 * B * (D + H) * G4
 
 PIN = True
 LEAD = 5
-XL = 2
 V_PAIRS = 3
+QB = [1, 1, 2, 4, 4, 4, 4, 4, 4, 4]
+SA_MOD = 0
 XBUFS = 4
 
 
@@ -46,6 +47,27 @@ def tile_lstmcell_t_kernel(
     hout = out_0.rearrange("(p t) n -> p t n", t=NT)
     cout = out_1.rearrange("(p t) n -> p t n", t=NT)
 
+    assert sum(QB) == NT
+    batch_of = {}
+    lo = 0
+    for bi, nb in enumerate(QB):
+        for t in range(lo, lo + nb):
+            batch_of[t] = (bi, lo, nb)
+        lo += nb
+    xstep = {}
+    qstep = {}
+    for t in range(NT):
+        st = 2 + t // 2 if t < 4 else t
+        xstep[st] = xstep.get(st, []) + [t]
+        bi, blo, nb = batch_of[t]
+        if t == blo + nb - 1:
+            sq = st if blo < 4 else st + 1
+            assert sq < blo + LEAD
+            qstep[sq] = qstep.get(sq, []) + [blo]
+
+    def on_scalar(t, h):
+        return SA_MOD > 0 and h == 1 and t % SA_MOD == SA_MOD - 1
+
     with ExitStack() as ctx:
         if PIN:
             ctx.enter_context(tc.manual_schedule())
@@ -65,11 +87,11 @@ def tile_lstmcell_t_kernel(
         wgrp = const.tile([P, 2, G4, 2], F32, name="wgrp", align_bytes=64)
         wc = const.tile([P, 2, G4], U32, name="wc", align_bytes=64)
         ws = const.tile([P, 2, G4], U8, name="ws", align_bytes=64)
-        h0raw = const.tile([P, NT, H], BF16, name="h0raw")
-        h0w = const.tile([P, NT, P], F32, name="h0w")
         c0sb = const.tile([P, NT, H], BF16, name="c0sb")
 
         xch = {}
+        h0r = {}
+        h0w = {}
         xts = {}
         grps = {}
         xcs = {}
@@ -85,8 +107,9 @@ def tile_lstmcell_t_kernel(
             xch[c] = xin.tile([P, CH, D], BF16, name="xch%d" % c, tag="xch")
             nc.sync.dma_start(out=xch[c][:], in_=xv[:, c * CH:(c + 1) * CH, :])
 
-        def load_h0(t0, t1):
-            nc.sync.dma_start(out=h0raw[:, t0:t1, :], in_=hv[:, t0:t1, :])
+        def load_h0(c):
+            h0r[c] = work.tile([P, CH, H], BF16, name="h0r%d" % c, tag="h0r", bufs=3)
+            nc.sync.dma_start(out=h0r[c][:], in_=hv[:, c * CH:(c + 1) * CH, :])
 
         def load_c0(t0, t1):
             nc.sync.dma_start(out=c0sb[:, t0:t1, :], in_=cv[:, t0:t1, :])
@@ -124,7 +147,7 @@ def tile_lstmcell_t_kernel(
         load_bias(nc.scalar, 1)
         load_wh(0)
         load_wh(1)
-        load_h0(0, 4)
+        load_h0(0)
         load_wh(2)
         load_wh(3)
         load_bias(nc.sync, 2)
@@ -134,14 +157,13 @@ def tile_lstmcell_t_kernel(
         load_x(0)
         load_w(2)
         load_w(3)
-        load_h0(4, 8)
+        load_h0(1)
         load_x(1)
         load_c0(0, 8)
         load_x(2)
-        load_h0(8, 16)
+        load_h0(2)
         load_x(3)
         load_c0(8, 16)
-        load_h0(16, 32)
         load_c0(16, 32)
         nc.scalar.activation(out=warm[:, 1:2], in_=warm[:, 0:1], func=AF.Sigmoid)
 
@@ -153,10 +175,13 @@ def tile_lstmcell_t_kernel(
             copy(out=whw[:, half(b)], in_=pb[:])
 
         def h0_tr(c, pb):
-            return [("t", pb, j, h0raw[:, c * CH + j, :].bitcast(F32)) for j in range(CH)]
+            return [("t", pb, j, h0r[c][:, j, :].bitcast(F32)) for j in range(CH)]
 
         def h0_copy(c, pb, copy):
-            copy(out=h0w[:, c * CH:(c + 1) * CH, :].rearrange("p t r -> p (t r)"), in_=pb[:])
+            h0w[c] = work.tile([P, CH, P], F32, name="h0w%d" % c, tag="h0w", bufs=3)
+            copy(out=h0w[c][:].rearrange("p t r -> p (t r)"), in_=pb[:])
+            if c + 3 < NCH:
+                load_h0(c + 3)
 
         def bias_bank(h, tag, copy):
             pb = bank(tag, "bp%d" % h)
@@ -166,14 +191,17 @@ def tile_lstmcell_t_kernel(
         def run(op):
             if op[0] == "t":
                 tr(op[1], op[2], op[3])
+            elif op[0] == "b":
+                t, h = op[1], op[2]
+                nc.tensor.matmul(out=ghs[(t, h)][:], lhsT=ones[:], rhs=brow[:, half(h)], start=False, stop=True)
             else:
                 t, h, e = op[1], op[2], op[3]
                 nc.tensor.matmul(
                     out=ghs[(t, h)][:],
-                    lhsT=pairs_view(h0w[:, t, :])[:, :, e],
+                    lhsT=pairs_view(h0w[t // CH][:, t % CH, :])[:, :, e],
                     rhs=pairs_view(whw[:, half(h)])[:, :, e],
                     start=(e == 0),
-                    stop=(e == 1),
+                    stop=(e == 1 and not on_scalar(t, h)),
                 )
 
         def weave(mm, trs):
@@ -215,26 +243,31 @@ def tile_lstmcell_t_kernel(
                 )
 
         def x_copy(t):
-            grps[t] = work.tile([P, 2, P, 2], F32, name="grp%d" % t, tag="grp", bufs=3, align_bytes=64)
-            nc.scalar.copy(out=grps[t][:], in_=grouped_read(xts[t]))
+            bi, blo, nb = batch_of[t]
+            if t == blo:
+                grps[blo] = work.tile([P, nb, 2, P, 2], F32, name="grp%d" % blo, tag="grp", bufs=2, align_bytes=64)
+            nc.scalar.copy(out=grps[blo][:, t - blo, :, :, :], in_=grouped_read(xts[t]))
 
-        def x_quant(t):
-            xcs[t] = work.tile([P, 2 * P], U32, name="xc%d" % t, tag="xc", bufs=XL + 2, align_bytes=64)
-            xss[t] = work.tile([P, 2 * P], U8, name="xs%d" % t, tag="xs", bufs=XL + 2, align_bytes=64)
+        def x_quant(blo):
+            nb = batch_of[blo][2]
+            xcs[blo] = work.tile([P, nb * 2 * P], U32, name="xc%d" % blo, tag="xc", bufs=3, align_bytes=64)
+            xss[blo] = work.tile([P, nb * 2 * P], U8, name="xs%d" % blo, tag="xs", bufs=3, align_bytes=64)
             nc.vector.quantize_mx(
-                out=xcs[t][:].bitcast(FP8X4),
-                scales=xss[t][:],
-                in_=grps[t][:].rearrange("p g r u -> p (g r u)").bitcast(BF16),
+                out=xcs[blo][:].bitcast(FP8X4),
+                scales=xss[blo][:],
+                in_=grps[blo][:].rearrange("p t g r u -> p (t g r u)").bitcast(BF16),
             )
 
         def m_passes(t):
+            blo = batch_of[t][1]
             for h in range(2):
                 gxs[(t, h)] = bank("gx", "gx%d_%d" % (t, h))
                 for g in range(2):
+                    col = ((t - blo) * 2 + g) * P
                     nc.tensor.matmul_mx(
                         out=gxs[(t, h)][:],
-                        lhsT=xcs[t][:, g * P:(g + 1) * P].bitcast(FP8X4),
-                        lhsT_scale=xss[t][:, g * P:(g + 1) * P],
+                        lhsT=xcs[blo][:, col:col + P].bitcast(FP8X4),
+                        lhsT_scale=xss[blo][:, col:col + P],
                         rhs=wc[:, g, half(h)].bitcast(FP8X4),
                         rhs_scale=ws[:, g, half(h)],
                         start=(g == 0),
@@ -242,7 +275,10 @@ def tile_lstmcell_t_kernel(
                     )
 
         def a_op(t, h):
-            nc.vector.tensor_tensor(out=tsbs[t][:, half(h)], in0=ghs[(t, h)][:], in1=bias[:, half(h)], op=ALU.add)
+            if on_scalar(t, h):
+                nc.scalar.copy(out=tsbs[t][:, half(h)], in_=ghs[(t, h)][:])
+            else:
+                nc.vector.tensor_tensor(out=tsbs[t][:, half(h)], in0=ghs[(t, h)][:], in1=bias[:, half(h)], op=ALU.add)
 
         def b_op(t, h):
             nc.vector.tensor_tensor(out=tsbs[t][:, half(h)], in0=gxs[(t, h)][:], in1=tsbs[t][:, half(h)], op=ALU.add)
@@ -277,37 +313,49 @@ def tile_lstmcell_t_kernel(
             d_eng(k).tensor_tensor(out=ht[:], in0=acts[k][:, :, 2 * H:3 * H], in1=tchs[k][:], op=ALU.mult)
             nc.sync.dma_start(out=hout[:, 2 * k:2 * k + 2, :], in_=ht[:])
 
+        def x_bank(t):
+            xts[t] = bank("xt", "xt%d" % t)
+            xw = xch[t // CH][:, t % CH, :].bitcast(F32)
+            return [("t", xts[t], q, xw[:, q * P:(q + 1) * P]) for q in range(4)]
+
+        def x_out(t):
+            x_copy(t)
+            if t % CH == CH - 1 and t // CH + XBUFS < NCH:
+                load_x(t // CH + XBUFS)
+
         for s in range(NT + LEAD):
             tM = s - LEAD
-            tX = tM + XL
-            tq = tX - 1
             mm = []
             trs = []
             hc = None
+            xt_now = xstep.get(s, [])
             if s < NT:
                 tsbs[s] = work.tile([P, G4], F32, name="tsb%d" % s, tag="tsb", bufs=LEAD + 3)
                 for h in range(2):
                     ghs[(s, h)] = bank("gh", "gh%d_%d" % (s, h))
-                mm = [("m", s, h, e) for h in range(2) for e in range(2)]
-            if 0 <= tX < NT:
-                xts[tX] = bank("xt", "xt%d" % tX)
-                xw = xch[tX // CH][:, tX % CH, :].bitcast(F32)
-                trs = trs + [("t", xts[tX], q, xw[:, q * P:(q + 1) * P]) for q in range(4)]
+                    mm = mm + [("m", s, h, 0), ("m", s, h, 1)]
+                    if on_scalar(s, h):
+                        mm = mm + [("b", s, h)]
+            if s >= 4:
+                for t in xt_now:
+                    trs = trs + x_bank(t)
             if s % CH == 2 and s + 2 < NT:
                 hc = (s + 2) // CH
                 hpb = bank("xt", "h0p%d" % hc)
                 trs = trs + h0_tr(hc, hpb)
             weave(mm, trs)
+            if hc is not None:
+                h0_copy(hc, hpb, nc.scalar.copy)
             if s < 4:
+                for t in xt_now:
+                    weave([], x_bank(t))
+                    x_out(t)
                 w_gate(s)
             if 0 <= tM:
                 m_passes(tM)
-            if 0 <= tX < NT:
-                x_copy(tX)
-                if tX % CH == CH - 1 and tX // CH + XBUFS < NCH:
-                    load_x(tX // CH + XBUFS)
-            if hc is not None:
-                h0_copy(hc, hpb, nc.scalar.copy)
+            if s >= 4:
+                for t in xt_now:
+                    x_out(t)
             if s < NT:
                 a_op(s, 0)
                 a_op(s, 1)
@@ -315,8 +363,8 @@ def tile_lstmcell_t_kernel(
                 w_quant(0)
             if s == LEAD - 1:
                 w_quant(1)
-            if 0 <= tq < NT:
-                x_quant(tq)
+            for blo in qstep.get(s, []):
+                x_quant(blo)
             if 0 <= tM:
                 b_op(tM, 0)
                 b_op(tM, 1)

@@ -21,11 +21,12 @@ NCH = NT // CH
 FLOPS = 2 * B * (D + H) * G4
 
 PIN = True
-LEAD = 5
-V_PAIRS = 3
-QB = [1, 1, 2, 4, 4, 4, 4, 4, 4, 4]
+LEAD = 4
+V_PAIRS = 2
+QB = [2] * 16
 SA_MOD = 0
 XBUFS = 4
+PSUM_BUFS = {"xt": 3, "gh": 2, "gx": 3}
 
 
 def tile_lstmcell_t_kernel(
@@ -54,17 +55,6 @@ def tile_lstmcell_t_kernel(
         for t in range(lo, lo + nb):
             batch_of[t] = (bi, lo, nb)
         lo += nb
-    xstep = {}
-    qstep = {}
-    for t in range(NT):
-        st = 2 + t // 2 if t < 4 else t
-        xstep[st] = xstep.get(st, []) + [t]
-        bi, blo, nb = batch_of[t]
-        if t == blo + nb - 1:
-            sq = st if blo < 4 else st + 1
-            assert sq < blo + LEAD
-            qstep[sq] = qstep.get(sq, []) + [blo]
-
     def on_scalar(t, h):
         return SA_MOD > 0 and h == 1 and t % SA_MOD == SA_MOD - 1
 
@@ -125,7 +115,7 @@ def tile_lstmcell_t_kernel(
             nc.sync.dma_start(out=wraw[g][:], in_=w_in[g].rearrange("(j p) k -> p j k", p=P))
 
         def bank(tag, name):
-            return psum.tile([P, HALF], F32, name=name, tag=tag, bufs=(2 if tag == "xt" else 3))
+            return psum.tile([P, HALF], F32, name=name, tag=tag, bufs=PSUM_BUFS[tag])
 
         def half(h):
             return slice(h * HALF, (h + 1) * HALF)
@@ -323,57 +313,55 @@ def tile_lstmcell_t_kernel(
             if t % CH == CH - 1 and t // CH + XBUFS < NCH:
                 load_x(t // CH + XBUFS)
 
-        for s in range(NT + LEAD):
+        def substep(s):
             tM = s - LEAD
-            mm = []
-            trs = []
-            hc = None
-            xt_now = xstep.get(s, [])
             if s < NT:
                 tsbs[s] = work.tile([P, G4], F32, name="tsb%d" % s, tag="tsb", bufs=LEAD + 3)
                 for h in range(2):
                     ghs[(s, h)] = bank("gh", "gh%d_%d" % (s, h))
-                    mm = mm + [("m", s, h, 0), ("m", s, h, 1)]
+                    run(("m", s, h, 0))
+                    run(("m", s, h, 1))
                     if on_scalar(s, h):
-                        mm = mm + [("b", s, h)]
-            if s >= 4:
-                for t in xt_now:
-                    trs = trs + x_bank(t)
+                        run(("b", s, h))
+                a_op(s, 0)
+                a_op(s, 1)
+            if s < 4:
+                w_gate(s)
+            if s == 1:
+                w_quant(0)
+            if s == 3:
+                w_quant(1)
+            if 0 <= tM:
+                m_passes(tM)
+                b_op(tM, 0)
+                b_op(tM, 1)
+                c_op(tM)
+
+        for s in range(0, NT + LEAD, 2):
+            tX = s - LEAD + 2
+            trs = []
+            hc = None
+            if 0 <= tX < NT:
+                trs = trs + x_bank(tX) + x_bank(tX + 1)
             if s % CH == 2 and s + 2 < NT:
                 hc = (s + 2) // CH
                 hpb = bank("xt", "h0p%d" % hc)
                 trs = trs + h0_tr(hc, hpb)
-            weave(mm, trs)
+            weave([], trs)
+            if 0 <= tX < NT:
+                x_out(tX)
+                x_out(tX + 1)
             if hc is not None:
                 h0_copy(hc, hpb, nc.scalar.copy)
-            if s < 4:
-                for t in xt_now:
-                    weave([], x_bank(t))
-                    x_out(t)
-                w_gate(s)
-            if 0 <= tM:
-                m_passes(tM)
-            if s >= 4:
-                for t in xt_now:
-                    x_out(t)
-            if s < NT:
-                a_op(s, 0)
-                a_op(s, 1)
-            if s == LEAD - 2:
-                w_quant(0)
-            if s == LEAD - 1:
-                w_quant(1)
-            for blo in qstep.get(s, []):
-                x_quant(blo)
-            if 0 <= tM:
-                b_op(tM, 0)
-                b_op(tM, 1)
-                c_op(tM)
-                if tM % 2 == 1:
-                    k = tM // 2
-                    d1(k)
-                    if k >= 1:
-                        tanh_c(k - 1)
-                        dh(k - 1)
+            substep(s)
+            if 0 <= tX < NT:
+                x_quant(tX)
+            substep(s + 1)
+            k = (s - LEAD) // 2
+            if 0 <= k:
+                d1(k)
+                if k >= 1:
+                    tanh_c(k - 1)
+                    dh(k - 1)
         tanh_c(NT // 2 - 1)
         dh(NT // 2 - 1)

@@ -21,12 +21,11 @@ NCH = NT // CH
 FLOPS = 2 * B * (D + H) * G4
 
 PIN = True
-LEAD = 4
-V_PAIRS = 2
-QB = [2] * 16
-SA_MOD = 0
+LEAD = 5
+XL = 2
+V_PAIRS = 3
 XBUFS = 4
-PSUM_BUFS = {"xt": 3, "gh": 2, "gx": 3}
+SA_MOD = 2
 
 
 def tile_lstmcell_t_kernel(
@@ -48,16 +47,6 @@ def tile_lstmcell_t_kernel(
     hout = out_0.rearrange("(p t) n -> p t n", t=NT)
     cout = out_1.rearrange("(p t) n -> p t n", t=NT)
 
-    assert sum(QB) == NT
-    batch_of = {}
-    lo = 0
-    for bi, nb in enumerate(QB):
-        for t in range(lo, lo + nb):
-            batch_of[t] = (bi, lo, nb)
-        lo += nb
-    def on_scalar(t, h):
-        return SA_MOD > 0 and h == 1 and t % SA_MOD == SA_MOD - 1
-
     with ExitStack() as ctx:
         if PIN:
             ctx.enter_context(tc.manual_schedule())
@@ -77,11 +66,11 @@ def tile_lstmcell_t_kernel(
         wgrp = const.tile([P, 2, G4, 2], F32, name="wgrp", align_bytes=64)
         wc = const.tile([P, 2, G4], U32, name="wc", align_bytes=64)
         ws = const.tile([P, 2, G4], U8, name="ws", align_bytes=64)
+        h0raw = const.tile([P, NT, H], BF16, name="h0raw")
+        h0w = const.tile([P, NT, P], F32, name="h0w")
         c0sb = const.tile([P, NT, H], BF16, name="c0sb")
 
         xch = {}
-        h0r = {}
-        h0w = {}
         xts = {}
         grps = {}
         xcs = {}
@@ -97,9 +86,8 @@ def tile_lstmcell_t_kernel(
             xch[c] = xin.tile([P, CH, D], BF16, name="xch%d" % c, tag="xch")
             nc.sync.dma_start(out=xch[c][:], in_=xv[:, c * CH:(c + 1) * CH, :])
 
-        def load_h0(c):
-            h0r[c] = work.tile([P, CH, H], BF16, name="h0r%d" % c, tag="h0r", bufs=3)
-            nc.sync.dma_start(out=h0r[c][:], in_=hv[:, c * CH:(c + 1) * CH, :])
+        def load_h0(t0, t1):
+            nc.sync.dma_start(out=h0raw[:, t0:t1, :], in_=hv[:, t0:t1, :])
 
         def load_c0(t0, t1):
             nc.sync.dma_start(out=c0sb[:, t0:t1, :], in_=cv[:, t0:t1, :])
@@ -115,7 +103,10 @@ def tile_lstmcell_t_kernel(
             nc.sync.dma_start(out=wraw[g][:], in_=w_in[g].rearrange("(j p) k -> p j k", p=P))
 
         def bank(tag, name):
-            return psum.tile([P, HALF], F32, name=name, tag=tag, bufs=PSUM_BUFS[tag])
+            return psum.tile([P, HALF], F32, name=name, tag=tag, bufs=(2 if tag == "xt" else 3))
+
+        def on_scalar(t, h):
+            return SA_MOD > 0 and h == 1 and t % SA_MOD == SA_MOD - 1
 
         def half(h):
             return slice(h * HALF, (h + 1) * HALF)
@@ -137,7 +128,7 @@ def tile_lstmcell_t_kernel(
         load_bias(nc.scalar, 1)
         load_wh(0)
         load_wh(1)
-        load_h0(0)
+        load_h0(0, 4)
         load_wh(2)
         load_wh(3)
         load_bias(nc.sync, 2)
@@ -147,13 +138,14 @@ def tile_lstmcell_t_kernel(
         load_x(0)
         load_w(2)
         load_w(3)
-        load_h0(1)
+        load_h0(4, 8)
         load_x(1)
         load_c0(0, 8)
         load_x(2)
-        load_h0(2)
+        load_h0(8, 16)
         load_x(3)
         load_c0(8, 16)
+        load_h0(16, 32)
         load_c0(16, 32)
         nc.scalar.activation(out=warm[:, 1:2], in_=warm[:, 0:1], func=AF.Sigmoid)
 
@@ -165,13 +157,10 @@ def tile_lstmcell_t_kernel(
             copy(out=whw[:, half(b)], in_=pb[:])
 
         def h0_tr(c, pb):
-            return [("t", pb, j, h0r[c][:, j, :].bitcast(F32)) for j in range(CH)]
+            return [("t", pb, j, h0raw[:, c * CH + j, :].bitcast(F32)) for j in range(CH)]
 
         def h0_copy(c, pb, copy):
-            h0w[c] = work.tile([P, CH, P], F32, name="h0w%d" % c, tag="h0w", bufs=3)
-            copy(out=h0w[c][:].rearrange("p t r -> p (t r)"), in_=pb[:])
-            if c + 3 < NCH:
-                load_h0(c + 3)
+            copy(out=h0w[:, c * CH:(c + 1) * CH, :].rearrange("p t r -> p (t r)"), in_=pb[:])
 
         def bias_bank(h, tag, copy):
             pb = bank(tag, "bp%d" % h)
@@ -182,13 +171,12 @@ def tile_lstmcell_t_kernel(
             if op[0] == "t":
                 tr(op[1], op[2], op[3])
             elif op[0] == "b":
-                t, h = op[1], op[2]
-                nc.tensor.matmul(out=ghs[(t, h)][:], lhsT=ones[:], rhs=brow[:, half(h)], start=False, stop=True)
+                nc.tensor.matmul(out=ghs[(op[1], op[2])][:], lhsT=ones[:], rhs=brow[:, half(op[2])], start=False, stop=True)
             else:
                 t, h, e = op[1], op[2], op[3]
                 nc.tensor.matmul(
                     out=ghs[(t, h)][:],
-                    lhsT=pairs_view(h0w[t // CH][:, t % CH, :])[:, :, e],
+                    lhsT=pairs_view(h0w[:, t, :])[:, :, e],
                     rhs=pairs_view(whw[:, half(h)])[:, :, e],
                     start=(e == 0),
                     stop=(e == 1 and not on_scalar(t, h)),
@@ -233,31 +221,26 @@ def tile_lstmcell_t_kernel(
                 )
 
         def x_copy(t):
-            bi, blo, nb = batch_of[t]
-            if t == blo:
-                grps[blo] = work.tile([P, nb, 2, P, 2], F32, name="grp%d" % blo, tag="grp", bufs=2, align_bytes=64)
-            nc.scalar.copy(out=grps[blo][:, t - blo, :, :, :], in_=grouped_read(xts[t]))
+            grps[t] = work.tile([P, 2, P, 2], F32, name="grp%d" % t, tag="grp", bufs=3, align_bytes=64)
+            nc.scalar.copy(out=grps[t][:], in_=grouped_read(xts[t]))
 
-        def x_quant(blo):
-            nb = batch_of[blo][2]
-            xcs[blo] = work.tile([P, nb * 2 * P], U32, name="xc%d" % blo, tag="xc", bufs=3, align_bytes=64)
-            xss[blo] = work.tile([P, nb * 2 * P], U8, name="xs%d" % blo, tag="xs", bufs=3, align_bytes=64)
+        def x_quant(t):
+            xcs[t] = work.tile([P, 2 * P], U32, name="xc%d" % t, tag="xc", bufs=XL + 2, align_bytes=64)
+            xss[t] = work.tile([P, 2 * P], U8, name="xs%d" % t, tag="xs", bufs=XL + 2, align_bytes=64)
             nc.vector.quantize_mx(
-                out=xcs[blo][:].bitcast(FP8X4),
-                scales=xss[blo][:],
-                in_=grps[blo][:].rearrange("p t g r u -> p (t g r u)").bitcast(BF16),
+                out=xcs[t][:].bitcast(FP8X4),
+                scales=xss[t][:],
+                in_=grps[t][:].rearrange("p g r u -> p (g r u)").bitcast(BF16),
             )
 
         def m_passes(t):
-            blo = batch_of[t][1]
             for h in range(2):
                 gxs[(t, h)] = bank("gx", "gx%d_%d" % (t, h))
                 for g in range(2):
-                    col = ((t - blo) * 2 + g) * P
                     nc.tensor.matmul_mx(
                         out=gxs[(t, h)][:],
-                        lhsT=xcs[blo][:, col:col + P].bitcast(FP8X4),
-                        lhsT_scale=xss[blo][:, col:col + P],
+                        lhsT=xcs[t][:, g * P:(g + 1) * P].bitcast(FP8X4),
+                        lhsT_scale=xss[t][:, g * P:(g + 1) * P],
                         rhs=wc[:, g, half(h)].bitcast(FP8X4),
                         rhs_scale=ws[:, g, half(h)],
                         start=(g == 0),
@@ -267,8 +250,8 @@ def tile_lstmcell_t_kernel(
         def a_op(t, h):
             if on_scalar(t, h):
                 nc.scalar.copy(out=tsbs[t][:, half(h)], in_=ghs[(t, h)][:])
-            else:
-                nc.vector.tensor_tensor(out=tsbs[t][:, half(h)], in0=ghs[(t, h)][:], in1=bias[:, half(h)], op=ALU.add)
+                return
+            nc.vector.tensor_tensor(out=tsbs[t][:, half(h)], in0=ghs[(t, h)][:], in1=bias[:, half(h)], op=ALU.add)
 
         def b_op(t, h):
             nc.vector.tensor_tensor(out=tsbs[t][:, half(h)], in0=gxs[(t, h)][:], in1=tsbs[t][:, half(h)], op=ALU.add)
@@ -303,65 +286,57 @@ def tile_lstmcell_t_kernel(
             d_eng(k).tensor_tensor(out=ht[:], in0=acts[k][:, :, 2 * H:3 * H], in1=tchs[k][:], op=ALU.mult)
             nc.sync.dma_start(out=hout[:, 2 * k:2 * k + 2, :], in_=ht[:])
 
-        def x_bank(t):
-            xts[t] = bank("xt", "xt%d" % t)
-            xw = xch[t // CH][:, t % CH, :].bitcast(F32)
-            return [("t", xts[t], q, xw[:, q * P:(q + 1) * P]) for q in range(4)]
-
-        def x_out(t):
-            x_copy(t)
-            if t % CH == CH - 1 and t // CH + XBUFS < NCH:
-                load_x(t // CH + XBUFS)
-
-        def substep(s):
+        for s in range(NT + LEAD):
             tM = s - LEAD
+            tX = tM + XL
+            tq = tX - 1
+            mm = []
+            trs = []
+            hc = None
             if s < NT:
                 tsbs[s] = work.tile([P, G4], F32, name="tsb%d" % s, tag="tsb", bufs=LEAD + 3)
                 for h in range(2):
                     ghs[(s, h)] = bank("gh", "gh%d_%d" % (s, h))
-                    run(("m", s, h, 0))
-                    run(("m", s, h, 1))
-                    if on_scalar(s, h):
-                        run(("b", s, h))
-                a_op(s, 0)
-                a_op(s, 1)
-            if s < 4:
-                w_gate(s)
-            if s == 1:
-                w_quant(0)
-            if s == 3:
-                w_quant(1)
-            if 0 <= tM:
-                m_passes(tM)
-                b_op(tM, 0)
-                b_op(tM, 1)
-                c_op(tM)
-
-        for s in range(0, NT + LEAD, 2):
-            tX = s - LEAD + 2
-            trs = []
-            hc = None
+                mm = [("m", s, h, e) for h in range(2) for e in range(2)]
+                if on_scalar(s, 1):
+                    mm = mm + [("b", s, 1)]
             if 0 <= tX < NT:
-                trs = trs + x_bank(tX) + x_bank(tX + 1)
+                xts[tX] = bank("xt", "xt%d" % tX)
+                xw = xch[tX // CH][:, tX % CH, :].bitcast(F32)
+                trs = trs + [("t", xts[tX], q, xw[:, q * P:(q + 1) * P]) for q in range(4)]
             if s % CH == 2 and s + 2 < NT:
                 hc = (s + 2) // CH
                 hpb = bank("xt", "h0p%d" % hc)
                 trs = trs + h0_tr(hc, hpb)
-            weave([], trs)
+            weave(mm, trs)
+            if s < 4:
+                w_gate(s)
+            if 0 <= tM:
+                m_passes(tM)
             if 0 <= tX < NT:
-                x_out(tX)
-                x_out(tX + 1)
+                x_copy(tX)
+                if tX % CH == CH - 1 and tX // CH + XBUFS < NCH:
+                    load_x(tX // CH + XBUFS)
             if hc is not None:
                 h0_copy(hc, hpb, nc.scalar.copy)
-            substep(s)
-            if 0 <= tX < NT:
-                x_quant(tX)
-            substep(s + 1)
-            k = (s - LEAD) // 2
-            if 0 <= k:
-                d1(k)
-                if k >= 1:
-                    tanh_c(k - 1)
-                    dh(k - 1)
+            if s < NT:
+                a_op(s, 0)
+                a_op(s, 1)
+            if s == LEAD - 2:
+                w_quant(0)
+            if s == LEAD - 1:
+                w_quant(1)
+            if 0 <= tq < NT:
+                x_quant(tq)
+            if 0 <= tM:
+                b_op(tM, 0)
+                b_op(tM, 1)
+                c_op(tM)
+                if tM % 2 == 1:
+                    k = tM // 2
+                    d1(k)
+                    if k >= 1:
+                        tanh_c(k - 1)
+                        dh(k - 1)
         tanh_c(NT // 2 - 1)
         dh(NT // 2 - 1)

@@ -23,9 +23,9 @@ FLOPS = 2 * B * (D + H) * G4
 PIN = True
 LEAD = 5
 XL = 2
-V_PAIRS = 3
+V_PAIRS = 16
 XBUFS = 4
-SA_MOD = 2
+SA_SKIP = 8
 
 
 def tile_lstmcell_t_kernel(
@@ -106,7 +106,7 @@ def tile_lstmcell_t_kernel(
             return psum.tile([P, HALF], F32, name=name, tag=tag, bufs=(2 if tag == "xt" else 3))
 
         def on_scalar(t, h):
-            return SA_MOD > 0 and h == 1 and t % SA_MOD == SA_MOD - 1
+            return SA_SKIP > 0 and h == 1 and t % SA_SKIP != 0
 
         def half(h):
             return slice(h * HALF, (h + 1) * HALF)
@@ -286,7 +286,7 @@ def tile_lstmcell_t_kernel(
             d_eng(k).tensor_tensor(out=ht[:], in0=acts[k][:, :, 2 * H:3 * H], in1=tchs[k][:], op=ALU.mult)
             nc.sync.dma_start(out=hout[:, 2 * k:2 * k + 2, :], in_=ht[:])
 
-        for s in range(NT + LEAD):
+        for s in range(NT + LEAD + 2):
             tM = s - LEAD
             tX = tM + XL
             tq = tX - 1
@@ -311,7 +311,7 @@ def tile_lstmcell_t_kernel(
             weave(mm, trs)
             if s < 4:
                 w_gate(s)
-            if 0 <= tM:
+            if 0 <= tM < NT:
                 m_passes(tM)
             if 0 <= tX < NT:
                 x_copy(tX)
@@ -322,21 +322,21 @@ def tile_lstmcell_t_kernel(
             if s < NT:
                 a_op(s, 0)
                 a_op(s, 1)
+            kd = None
+            if tM - 1 >= 0 and (tM - 1) % 2 == 1:
+                kd = (tM - 1) // 2
+                d1(kd)
+            if tM - 2 >= 0 and (tM - 2) % 2 == 1:
+                dh((tM - 2) // 2)
             if s == LEAD - 2:
                 w_quant(0)
             if s == LEAD - 1:
                 w_quant(1)
             if 0 <= tq < NT:
                 x_quant(tq)
-            if 0 <= tM:
+            if 0 <= tM < NT:
                 b_op(tM, 0)
                 b_op(tM, 1)
                 c_op(tM)
-                if tM % 2 == 1:
-                    k = tM // 2
-                    d1(k)
-                    if k >= 1:
-                        tanh_c(k - 1)
-                        dh(k - 1)
-        tanh_c(NT // 2 - 1)
-        dh(NT // 2 - 1)
+            if kd is not None:
+                tanh_c(kd)

@@ -21,11 +21,11 @@ NCH = NT // CH
 FLOPS = 2 * B * (D + H) * G4
 
 PIN = True
-LEAD = 5
+LEAD = 1
 XL = 2
-V_PAIRS = 16
+V_PAIRS = 1
 XBUFS = 4
-SA_SKIP = 8
+MFIRST = False
 
 
 def tile_lstmcell_t_kernel(
@@ -63,7 +63,7 @@ def tile_lstmcell_t_kernel(
         whraw = [const.tile([P, 2, H], BF16, name="whraw%d" % g) for g in range(4)]
         whw = const.tile([P, G4], F32, name="whw")
         wraw = [const.tile([P, 2, D], BF16, name="wraw%d" % g) for g in range(4)]
-        wgrp = const.tile([P, 2, G4, 2], F32, name="wgrp", align_bytes=64)
+        wgs = [const.tile([P, 2, P, 2], F32, name="wg%d" % n, align_bytes=64) for n in range(8)]
         wc = const.tile([P, 2, G4], U32, name="wc", align_bytes=64)
         ws = const.tile([P, 2, G4], U8, name="ws", align_bytes=64)
         h0raw = const.tile([P, NT, H], BF16, name="h0raw")
@@ -82,9 +82,13 @@ def tile_lstmcell_t_kernel(
         cts = {}
         tchs = {}
 
-        def load_x(c):
+        def load_x(c, parts=1):
             xch[c] = xin.tile([P, CH, D], BF16, name="xch%d" % c, tag="xch")
-            nc.sync.dma_start(out=xch[c][:], in_=xv[:, c * CH:(c + 1) * CH, :])
+            n = CH // parts
+            return [(xch[c][:, i * n:(i + 1) * n, :], xv[:, c * CH + i * n:c * CH + (i + 1) * n, :]) for i in range(parts)]
+
+        def dma(pair):
+            nc.sync.dma_start(out=pair[0], in_=pair[1])
 
         def load_h0(t0, t1):
             nc.sync.dma_start(out=h0raw[:, t0:t1, :], in_=hv[:, t0:t1, :])
@@ -106,7 +110,7 @@ def tile_lstmcell_t_kernel(
             return psum.tile([P, HALF], F32, name=name, tag=tag, bufs=(2 if tag == "xt" else 3))
 
         def on_scalar(t, h):
-            return SA_SKIP > 0 and h == 1 and t % SA_SKIP != 0
+            return h == 1 and t % 8 != 0
 
         def half(h):
             return slice(h * HALF, (h + 1) * HALF)
@@ -124,26 +128,26 @@ def tile_lstmcell_t_kernel(
         nc.vector.memset(warm[:], 0.0)
         nc.vector.memset(brow[:], 0.0)
         nc.vector.memset(ones[:], 1.0)
-        load_bias(nc.scalar, 0)
-        load_bias(nc.scalar, 1)
         load_wh(0)
         load_wh(1)
         load_h0(0, 4)
         load_wh(2)
         load_wh(3)
-        load_bias(nc.sync, 2)
-        load_bias(nc.sync, 3)
         load_w(0)
         load_w(1)
-        load_x(0)
+        x0 = load_x(0, 2)
+        dma(x0[0])
+        for g in range(4):
+            load_bias(nc.sync, g)
         load_w(2)
         load_w(3)
+        dma(x0[1])
         load_h0(4, 8)
-        load_x(1)
+        dma(load_x(1)[0])
         load_c0(0, 8)
-        load_x(2)
+        dma(load_x(2)[0])
         load_h0(8, 16)
-        load_x(3)
+        dma(load_x(3)[0])
         load_c0(8, 16)
         load_h0(16, 32)
         load_c0(16, 32)
@@ -195,29 +199,19 @@ def tile_lstmcell_t_kernel(
             for op in trs[i:]:
                 run(op)
 
-        wh_bank(0, "xt", nc.vector.tensor_copy)
-        pb0 = bank("xt", "h0p0")
-        weave([], h0_tr(0, pb0))
-        h0_copy(0, pb0, nc.scalar.copy)
-        bias_bank(0, "gx", nc.vector.tensor_copy)
-        wh_bank(1, "gx", nc.scalar.copy)
-        bias_bank(1, "gx", nc.vector.tensor_copy)
+        def w_tile(n, tag, copy):
+            pb = bank(tag, "wp%d" % n)
+            ww = wraw[n // 2][:, n % 2, :].bitcast(F32)
+            for q in range(4):
+                tr(pb, q, ww[:, q * P:(q + 1) * P])
+            copy(out=wgs[n][:], in_=grouped_read(pb))
 
-        def w_gate(g):
-            for j in range(2):
-                pb = bank("gx", "wp%d_%d" % (g, j))
-                ww = wraw[g][:, j, :].bitcast(F32)
-                for q in range(4):
-                    tr(pb, q, ww[:, q * P:(q + 1) * P])
-                n0 = g * H + j * P
-                nc.scalar.copy(out=wgrp[:, :, n0:n0 + P, :], in_=grouped_read(pb))
-
-        def w_quant(h):
+        def w_quant(n):
             for g in range(2):
                 nc.vector.quantize_mx(
-                    out=wc[:, g, half(h)].bitcast(FP8X4),
-                    scales=ws[:, g, half(h)],
-                    in_=wgrp[:, g, half(h), :].rearrange("p n u -> p (n u)").bitcast(BF16),
+                    out=wc[:, g, n * P:(n + 1) * P].bitcast(FP8X4),
+                    scales=ws[:, g, n * P:(n + 1) * P],
+                    in_=wgs[n][:, g, :, :].rearrange("p r u -> p (r u)").bitcast(BF16),
                 )
 
         def x_copy(t):
@@ -281,62 +275,149 @@ def tile_lstmcell_t_kernel(
             tchs[k] = work.tile([P, 2, H], F32, name="tch%d" % k, tag="tch", bufs=2)
             nc.scalar.activation(out=tchs[k][:], in_=cts[k][:], func=AF.Tanh)
 
-        def dh(k):
+        def dh(k, eng=None):
             ht = work.tile([P, 2, H], F32, name="ht%d" % k, tag="ht", bufs=3)
-            d_eng(k).tensor_tensor(out=ht[:], in0=acts[k][:, :, 2 * H:3 * H], in1=tchs[k][:], op=ALU.mult)
+            (eng or d_eng(k)).tensor_tensor(out=ht[:], in0=acts[k][:, :, 2 * H:3 * H], in1=tchs[k][:], op=ALU.mult)
             nc.sync.dma_start(out=hout[:, 2 * k:2 * k + 2, :], in_=ht[:])
 
-        for s in range(NT + LEAD + 2):
+        p1s = {}
+
+        def c_half(t, h):
+            if t % 2 == 0 and h == 0:
+                acts[t // 2] = work.tile([P, 2, G4], F32, name="act%d" % (t // 2), tag="act", bufs=3)
+            a = acts[t // 2]
+            j = t % 2
+            if h == 0:
+                nc.scalar.activation(out=a[:, j, 0:2 * H], in_=tsbs[t][:, 0:2 * H], func=AF.Sigmoid)
+            else:
+                nc.scalar.activation(out=a[:, j, 3 * H:G4], in_=tsbs[t][:, 3 * H:G4], func=AF.Tanh)
+                nc.scalar.activation(out=a[:, j, 2 * H:3 * H], in_=tsbs[t][:, 2 * H:3 * H], func=AF.Sigmoid)
+
+        def p1t(t):
+            p1s[t] = work.tile([P, H], F32, name="q1_%d" % t, tag="q1", bufs=2)
+            nc.vector.tensor_tensor(out=p1s[t][:], in0=acts[t // 2][:, t % 2, H:2 * H], in1=c0sb[:, t, :], op=ALU.mult)
+
+        def p2ct(t):
+            a = acts[t // 2]
+            j = t % 2
+            p2 = work.tile([P, H], F32, name="q2_%d" % t, tag="q2", bufs=2)
+            cts[("t", t)] = work.tile([P, H], F32, name="cu%d" % t, tag="cu", bufs=2)
+            nc.vector.tensor_tensor(out=p2[:], in0=a[:, j, 0:H], in1=a[:, j, 3 * H:G4], op=ALU.mult)
+            nc.vector.tensor_tensor(out=cts[("t", t)][:], in0=p1s[t][:], in1=p2[:], op=ALU.add)
+            nc.sync.dma_start(out=cout[:, t, :], in_=cts[("t", t)][:])
+
+        def tanh_ct(t):
+            tchs[("t", t)] = work.tile([P, H], F32, name="tu%d" % t, tag="tu", bufs=2)
+            nc.scalar.activation(out=tchs[("t", t)][:], in_=cts[("t", t)][:], func=AF.Tanh)
+
+        def dht(t):
+            ht = work.tile([P, H], F32, name="hu%d" % t, tag="hu", bufs=2)
+            nc.vector.tensor_tensor(out=ht[:], in0=acts[t // 2][:, t % 2, 2 * H:3 * H], in1=tchs[("t", t)][:], op=ALU.mult)
+            nc.sync.dma_start(out=hout[:, t, :], in_=ht[:])
+
+        def x_stage(t):
+            xts[t] = bank("xt", "xt%d" % t)
+            xw = xch[t // CH][:, t % CH, :].bitcast(F32)
+            return [("t", xts[t], q, xw[:, q * P:(q + 1) * P]) for q in range(4)]
+
+        def x_done(t):
+            x_copy(t)
+            if t % CH == CH - 1 and t // CH + XBUFS < NCH:
+                dma(load_x(t // CH + XBUFS)[0])
+
+        def h_stage(s):
+            tsbs[s] = work.tile([P, G4], F32, name="tsb%d" % s, tag="tsb", bufs=LEAD + 3)
+            for h in range(2):
+                ghs[(s, h)] = bank("gh", "gh%d_%d" % (s, h))
+            mm = [("m", s, h, e) for h in range(2) for e in range(2)]
+            if on_scalar(s, 1):
+                mm = mm + [("b", s, 1)]
+            return mm
+
+        vcopy = nc.vector.tensor_copy
+        scopy = nc.scalar.copy
+        wh_bank(0, "xt", vcopy)
+        pb0 = bank("xt", "h0p0")
+        weave([], h0_tr(0, pb0))
+        h0_copy(0, pb0, scopy)
+        wh_bank(1, "gx", vcopy)
+        for s in range(LEAD):
+            weave(h_stage(s), [])
+        for n in range(4):
+            w_tile(n, "gx" if n % 2 == 0 else "xt", scopy if n % 2 == 0 else vcopy)
+        for n in range(4):
+            w_quant(n)
+        for t in range(XL):
+            weave([], x_stage(t))
+            x_done(t)
+        bias_bank(0, "gx", vcopy)
+        bias_bank(1, "gx", scopy)
+        for s in range(LEAD):
+            a_op(s, 0)
+            a_op(s, 1)
+        for n in range(4, 8):
+            w_tile(n, "gx" if n % 2 == 0 else "xt", scopy if n % 2 == 0 else vcopy)
+        for t in range(XL - 1):
+            x_quant(t)
+        for n in range(4, 8):
+            w_quant(n)
+
+        NG = NT // 2 - V_PAIRS
+        for s in range(LEAD, NT + LEAD):
             tM = s - LEAD
             tX = tM + XL
             tq = tX - 1
             mm = []
             trs = []
             hc = None
+            if MFIRST:
+                m_passes(tM)
             if s < NT:
-                tsbs[s] = work.tile([P, G4], F32, name="tsb%d" % s, tag="tsb", bufs=LEAD + 3)
-                for h in range(2):
-                    ghs[(s, h)] = bank("gh", "gh%d_%d" % (s, h))
-                mm = [("m", s, h, e) for h in range(2) for e in range(2)]
-                if on_scalar(s, 1):
-                    mm = mm + [("b", s, 1)]
-            if 0 <= tX < NT:
-                xts[tX] = bank("xt", "xt%d" % tX)
-                xw = xch[tX // CH][:, tX % CH, :].bitcast(F32)
-                trs = trs + [("t", xts[tX], q, xw[:, q * P:(q + 1) * P]) for q in range(4)]
+                mm = h_stage(s)
+            if tX < NT:
+                trs = trs + x_stage(tX)
             if s % CH == 2 and s + 2 < NT:
                 hc = (s + 2) // CH
                 hpb = bank("xt", "h0p%d" % hc)
                 trs = trs + h0_tr(hc, hpb)
             weave(mm, trs)
-            if s < 4:
-                w_gate(s)
-            if 0 <= tM < NT:
+            if not MFIRST:
                 m_passes(tM)
-            if 0 <= tX < NT:
-                x_copy(tX)
-                if tX % CH == CH - 1 and tX // CH + XBUFS < NCH:
-                    load_x(tX // CH + XBUFS)
+            if tX < NT:
+                x_done(tX)
             if hc is not None:
-                h0_copy(hc, hpb, nc.scalar.copy)
-            if s < NT:
-                a_op(s, 0)
-                a_op(s, 1)
-            kd = None
-            if tM - 1 >= 0 and (tM - 1) % 2 == 1:
-                kd = (tM - 1) // 2
-                d1(kd)
-            if tM - 2 >= 0 and (tM - 2) % 2 == 1:
-                dh((tM - 2) // 2)
-            if s == LEAD - 2:
-                w_quant(0)
-            if s == LEAD - 1:
-                w_quant(1)
-            if 0 <= tq < NT:
-                x_quant(tq)
-            if 0 <= tM < NT:
+                h0_copy(hc, hpb, scopy)
+            if MFIRST:
                 b_op(tM, 0)
                 b_op(tM, 1)
                 c_op(tM)
-            if kd is not None:
-                tanh_c(kd)
+            if s < NT:
+                a_op(s, 0)
+                a_op(s, 1)
+            if tq < NT:
+                x_quant(tq)
+            if tM < 2 * NG:
+                b_op(tM, 0)
+                b_op(tM, 1)
+                c_op(tM)
+            else:
+                b_op(tM, 0)
+                c_half(tM, 0)
+                b_op(tM, 1)
+                c_half(tM, 1)
+            if tM % 2 == 1:
+                k = tM // 2
+                if k < NG:
+                    d1(k)
+                if 1 <= k < NG:
+                    tanh_c(k - 1)
+                    dh(k - 1)
+        tail = list(range(2 * NG, NT))
+        for t in tail:
+            p1t(t)
+            p2ct(t)
+            tanh_ct(t)
+        tanh_c(NG - 1)
+        for t in tail:
+            dht(t)
+        dh(NG - 1, nc.vector)

@@ -350,15 +350,16 @@ def tile_lstmcell_t_kernel(
         for t in range(XL):
             weave([], x_stage(t))
             x_done(t)
+        for t in range(XL - 1):
+            x_quant(t)
         bias_bank(0, "gx", vcopy)
         bias_bank(1, "gx", scopy)
         for s in range(LEAD):
             a_op(s, 0)
             a_op(s, 1)
+        w2 = "ssss"
         for n in range(4, 8):
-            w_tile(n, "gx" if n % 2 == 0 else "xt", scopy if n % 2 == 0 else vcopy)
-        for t in range(XL - 1):
-            x_quant(t)
+            w_tile(n, "gx" if n % 2 == 0 else "xt", scopy if w2[n - 4] == "s" else vcopy)
         for n in range(4, 8):
             w_quant(n)
 

@@ -107,10 +107,10 @@ def tile_lstmcell_t_kernel(
             nc.sync.dma_start(out=wraw[g][:], in_=w_in[g].rearrange("(j p) k -> p j k", p=P))
 
         def bank(tag, name):
-            return psum.tile([P, HALF], F32, name=name, tag=tag, bufs=(2 if tag == "xt" else 3))
+            return psum.tile([P, HALF], F32, name=name, tag=tag, bufs={"xt": 3, "gh": 3, "gx": 2}[tag])
 
         def on_scalar(t, h):
-            return h == 1 and t % 8 != 0
+            return h == 1 and t % 4 != 0
 
         def half(h):
             return slice(h * HALF, (h + 1) * HALF)
@@ -350,16 +350,15 @@ def tile_lstmcell_t_kernel(
         for t in range(XL):
             weave([], x_stage(t))
             x_done(t)
-        for t in range(XL - 1):
-            x_quant(t)
         bias_bank(0, "gx", vcopy)
         bias_bank(1, "gx", scopy)
         for s in range(LEAD):
             a_op(s, 0)
             a_op(s, 1)
-        w2 = "ssss"
         for n in range(4, 8):
-            w_tile(n, "gx" if n % 2 == 0 else "xt", scopy if w2[n - 4] == "s" else vcopy)
+            w_tile(n, "gx" if n % 2 == 0 else "xt", scopy if n % 2 == 0 else vcopy)
+        for t in range(XL - 1):
+            x_quant(t)
         for n in range(4, 8):
             w_quant(n)
 

@@ -26,6 +26,8 @@ XL = 2
 V_PAIRS = 1
 XBUFS = 4
 MFIRST = False
+HLAG = 2
+NBMOD = 4
 
 
 def tile_lstmcell_t_kernel(
@@ -63,7 +65,7 @@ def tile_lstmcell_t_kernel(
         whraw = [const.tile([P, 2, H], BF16, name="whraw%d" % g) for g in range(4)]
         whw = const.tile([P, G4], F32, name="whw")
         wraw = [const.tile([P, 2, D], BF16, name="wraw%d" % g) for g in range(4)]
-        wgs = [const.tile([P, 2, P, 2], F32, name="wg%d" % n, align_bytes=64) for n in range(8)]
+        wgs = {}
         wc = const.tile([P, 2, G4], U32, name="wc", align_bytes=64)
         ws = const.tile([P, 2, G4], U8, name="ws", align_bytes=64)
         h0raw = const.tile([P, NT, H], BF16, name="h0raw")
@@ -110,7 +112,7 @@ def tile_lstmcell_t_kernel(
             return psum.tile([P, HALF], F32, name=name, tag=tag, bufs={"xt": 3, "gh": 3, "gx": 2}[tag])
 
         def on_scalar(t, h):
-            return h == 1 and t % 4 != 0
+            return h == 1 and t % NBMOD != 0
 
         def half(h):
             return slice(h * HALF, (h + 1) * HALF)
@@ -204,6 +206,7 @@ def tile_lstmcell_t_kernel(
             ww = wraw[n // 2][:, n % 2, :].bitcast(F32)
             for q in range(4):
                 tr(pb, q, ww[:, q * P:(q + 1) * P])
+            wgs[n] = work.tile([P, 2, P, 2], F32, name="wg%d" % n, tag="wg", bufs=4, align_bytes=64)
             copy(out=wgs[n][:], in_=grouped_read(pb))
 
         def w_quant(n):
@@ -215,16 +218,17 @@ def tile_lstmcell_t_kernel(
                 )
 
         def x_copy(t):
-            grps[t] = work.tile([P, 2, P, 2], F32, name="grp%d" % t, tag="grp", bufs=3, align_bytes=64)
-            nc.scalar.copy(out=grps[t][:], in_=grouped_read(xts[t]))
+            if t % 2 == 0:
+                grps[t // 2] = work.tile([P, 2, 2, P, 2], F32, name="grp%d" % (t // 2), tag="grp", bufs=2, align_bytes=64)
+            nc.scalar.copy(out=grps[t // 2][:, t % 2], in_=grouped_read(xts[t]))
 
-        def x_quant(t):
-            xcs[t] = work.tile([P, 2 * P], U32, name="xc%d" % t, tag="xc", bufs=XL + 2, align_bytes=64)
-            xss[t] = work.tile([P, 2 * P], U8, name="xs%d" % t, tag="xs", bufs=XL + 2, align_bytes=64)
+        def x_quant(q):
+            xcs[q] = work.tile([P, 4 * P], U32, name="xc%d" % q, tag="xc", bufs=3, align_bytes=64)
+            xss[q] = work.tile([P, 4 * P], U8, name="xs%d" % q, tag="xs", bufs=3, align_bytes=64)
             nc.vector.quantize_mx(
-                out=xcs[t][:].bitcast(FP8X4),
-                scales=xss[t][:],
-                in_=grps[t][:].rearrange("p g r u -> p (g r u)").bitcast(BF16),
+                out=xcs[q][:].bitcast(FP8X4),
+                scales=xss[q][:],
+                in_=grps[q][:].rearrange("p t g r u -> p (t g r u)").bitcast(BF16),
             )
 
         def m_passes(t):
@@ -233,8 +237,8 @@ def tile_lstmcell_t_kernel(
                 for g in range(2):
                     nc.tensor.matmul_mx(
                         out=gxs[(t, h)][:],
-                        lhsT=xcs[t][:, g * P:(g + 1) * P].bitcast(FP8X4),
-                        lhsT_scale=xss[t][:, g * P:(g + 1) * P],
+                        lhsT=xcs[t // 2][:, (2 * (t % 2) + g) * P:(2 * (t % 2) + g + 1) * P].bitcast(FP8X4),
+                        lhsT_scale=xss[t // 2][:, (2 * (t % 2) + g) * P:(2 * (t % 2) + g + 1) * P],
                         rhs=wc[:, g, half(h)].bitcast(FP8X4),
                         rhs_scale=ws[:, g, half(h)],
                         start=(g == 0),
@@ -252,7 +256,7 @@ def tile_lstmcell_t_kernel(
 
         def c_op(t):
             if t % 2 == 0:
-                acts[t // 2] = work.tile([P, 2, G4], F32, name="act%d" % (t // 2), tag="act", bufs=3)
+                acts[t // 2] = work.tile([P, 2, G4], F32, name="act%d" % (t // 2), tag="act", bufs=4)
             a = acts[t // 2]
             nc.scalar.activation(out=a[:, t % 2, 0:3 * H], in_=tsbs[t][:, 0:3 * H], func=AF.Sigmoid)
             nc.scalar.activation(out=a[:, t % 2, 3 * H:G4], in_=tsbs[t][:, 3 * H:G4], func=AF.Tanh)
@@ -272,7 +276,7 @@ def tile_lstmcell_t_kernel(
             nc.sync.dma_start(out=cout[:, 2 * k:2 * k + 2, :], in_=cts[k][:])
 
         def tanh_c(k):
-            tchs[k] = work.tile([P, 2, H], F32, name="tch%d" % k, tag="tch", bufs=2)
+            tchs[k] = work.tile([P, 2, H], F32, name="tch%d" % k, tag="tch", bufs=3)
             nc.scalar.activation(out=tchs[k][:], in_=cts[k][:], func=AF.Tanh)
 
         def dh(k, eng=None):
@@ -284,7 +288,7 @@ def tile_lstmcell_t_kernel(
 
         def c_half(t, h):
             if t % 2 == 0 and h == 0:
-                acts[t // 2] = work.tile([P, 2, G4], F32, name="act%d" % (t // 2), tag="act", bufs=3)
+                acts[t // 2] = work.tile([P, 2, G4], F32, name="act%d" % (t // 2), tag="act", bufs=4)
             a = acts[t // 2]
             j = t % 2
             if h == 0:
@@ -294,24 +298,24 @@ def tile_lstmcell_t_kernel(
                 nc.scalar.activation(out=a[:, j, 2 * H:3 * H], in_=tsbs[t][:, 2 * H:3 * H], func=AF.Sigmoid)
 
         def p1t(t):
-            p1s[t] = work.tile([P, H], F32, name="q1_%d" % t, tag="q1", bufs=2)
+            p1s[t] = work.tile([P, H], F32, name="q1_%d" % t, tag="p1", bufs=2)
             nc.vector.tensor_tensor(out=p1s[t][:], in0=acts[t // 2][:, t % 2, H:2 * H], in1=c0sb[:, t, :], op=ALU.mult)
 
         def p2ct(t):
             a = acts[t // 2]
             j = t % 2
-            p2 = work.tile([P, H], F32, name="q2_%d" % t, tag="q2", bufs=2)
-            cts[("t", t)] = work.tile([P, H], F32, name="cu%d" % t, tag="cu", bufs=2)
+            p2 = work.tile([P, H], F32, name="q2_%d" % t, tag="p2", bufs=2)
+            cts[("t", t)] = work.tile([P, H], F32, name="cu%d" % t, tag="ct", bufs=3)
             nc.vector.tensor_tensor(out=p2[:], in0=a[:, j, 0:H], in1=a[:, j, 3 * H:G4], op=ALU.mult)
             nc.vector.tensor_tensor(out=cts[("t", t)][:], in0=p1s[t][:], in1=p2[:], op=ALU.add)
             nc.sync.dma_start(out=cout[:, t, :], in_=cts[("t", t)][:])
 
         def tanh_ct(t):
-            tchs[("t", t)] = work.tile([P, H], F32, name="tu%d" % t, tag="tu", bufs=2)
+            tchs[("t", t)] = work.tile([P, H], F32, name="tu%d" % t, tag="tch", bufs=3)
             nc.scalar.activation(out=tchs[("t", t)][:], in_=cts[("t", t)][:], func=AF.Tanh)
 
         def dht(t):
-            ht = work.tile([P, H], F32, name="hu%d" % t, tag="hu", bufs=2)
+            ht = work.tile([P, H], F32, name="hu%d" % t, tag="ht", bufs=3)
             nc.vector.tensor_tensor(out=ht[:], in0=acts[t // 2][:, t % 2, 2 * H:3 * H], in1=tchs[("t", t)][:], op=ALU.mult)
             nc.sync.dma_start(out=hout[:, t, :], in_=ht[:])
 
@@ -357,8 +361,7 @@ def tile_lstmcell_t_kernel(
             a_op(s, 1)
         for n in range(4, 8):
             w_tile(n, "gx" if n % 2 == 0 else "xt", scopy if n % 2 == 0 else vcopy)
-        for t in range(XL - 1):
-            x_quant(t)
+        x_quant(0)
         for n in range(4, 8):
             w_quant(n)
 
@@ -394,8 +397,6 @@ def tile_lstmcell_t_kernel(
             if s < NT:
                 a_op(s, 0)
                 a_op(s, 1)
-            if tq < NT:
-                x_quant(tq)
             if tM < 2 * NG:
                 b_op(tM, 0)
                 b_op(tM, 1)
@@ -407,17 +408,20 @@ def tile_lstmcell_t_kernel(
                 c_half(tM, 1)
             if tM % 2 == 1:
                 k = tM // 2
+                if k + 1 < NT // 2:
+                    x_quant(k + 1)
+                if 0 <= k - HLAG < NG:
+                    dh(k - HLAG, nc.vector)
                 if k < NG:
                     d1(k)
-                if 1 <= k < NG:
+                if 1 <= k <= NG:
                     tanh_c(k - 1)
-                    dh(k - 1)
         tail = list(range(2 * NG, NT))
         for t in tail:
             p1t(t)
             p2ct(t)
             tanh_ct(t)
-        tanh_c(NG - 1)
         for t in tail:
             dht(t)
-        dh(NG - 1, nc.vector)
+        for k in range(NT // 2 - HLAG, NG):
+            dh(k, nc.vector)

@@ -27,7 +27,7 @@ V_PAIRS = 1
 XBUFS = 4
 MFIRST = False
 HLAG = 2
-NBMOD = 4
+NBMOD = 2
 
 
 def tile_lstmcell_t_kernel(

@@ -368,32 +368,28 @@ def tile_lstmcell_t_kernel(
         NG = NT // 2 - V_PAIRS
         for s in range(LEAD, NT + LEAD):
             tM = s - LEAD
-            tX = tM + XL
-            tq = tX - 1
+            if tM < 2:
+                x_now = [2 * tM + 2, 2 * tM + 3]
+            else:
+                x_now = [tM + 4]
+            x_now = [t for t in x_now if t < NT]
             mm = []
             trs = []
             hc = None
-            if MFIRST:
-                m_passes(tM)
             if s < NT:
                 mm = h_stage(s)
-            if tX < NT:
-                trs = trs + x_stage(tX)
+            for t in x_now:
+                trs = trs + x_stage(t)
             if s % CH == 2 and s + 2 < NT:
                 hc = (s + 2) // CH
                 hpb = bank("xt", "h0p%d" % hc)
                 trs = trs + h0_tr(hc, hpb)
             weave(mm, trs)
-            if not MFIRST:
-                m_passes(tM)
-            if tX < NT:
-                x_done(tX)
+            m_passes(tM)
+            for t in x_now:
+                x_done(t)
             if hc is not None:
                 h0_copy(hc, hpb, scopy)
-            if MFIRST:
-                b_op(tM, 0)
-                b_op(tM, 1)
-                c_op(tM)
             if s < NT:
                 a_op(s, 0)
                 a_op(s, 1)
@@ -408,8 +404,10 @@ def tile_lstmcell_t_kernel(
                 c_half(tM, 1)
             if tM % 2 == 1:
                 k = tM // 2
-                if k + 1 < NT // 2:
-                    x_quant(k + 1)
+                if k == 0:
+                    x_quant(1)
+                if k + 2 < NT // 2:
+                    x_quant(k + 2)
                 if 0 <= k - HLAG < NG:
                     dh(k - HLAG, nc.vector)
                 if k < NG:

@@ -272,7 +272,17 @@ def tile_lstmcell_t_kernel(
             cts[k] = work.tile([P, 2, H], F32, name="ct%d" % k, tag="ct", bufs=3)
             eng.tensor_tensor(out=p1[:], in0=a[:, :, H:2 * H], in1=c0sb[:, 2 * k:2 * k + 2, :], op=ALU.mult)
             eng.tensor_tensor(out=p2[:], in0=a[:, :, 0:H], in1=a[:, :, 3 * H:G4], op=ALU.mult)
+            if k == NG - 1:
+                late_ct.append((k, p1, p2))
+                return
             eng.tensor_tensor(out=cts[k][:], in0=p1[:], in1=p2[:], op=ALU.add)
+            nc.sync.dma_start(out=cout[:, 2 * k:2 * k + 2, :], in_=cts[k][:])
+
+        late_ct = []
+
+        def ct_late():
+            k, p1, p2 = late_ct[0]
+            nc.vector.tensor_tensor(out=cts[k][:], in0=p1[:], in1=p2[:], op=ALU.add)
             nc.sync.dma_start(out=cout[:, 2 * k:2 * k + 2, :], in_=cts[k][:])
 
         def tanh_c(k):
@@ -298,24 +308,28 @@ def tile_lstmcell_t_kernel(
                 nc.scalar.activation(out=a[:, j, 2 * H:3 * H], in_=tsbs[t][:, 2 * H:3 * H], func=AF.Sigmoid)
 
         def p1t(t):
-            p1s[t] = work.tile([P, H], F32, name="q1_%d" % t, tag="p1", bufs=2)
+            p1s[t] = work.tile([P, H], F32, name="q1_%d" % t, tag="q1", bufs=2)
             nc.vector.tensor_tensor(out=p1s[t][:], in0=acts[t // 2][:, t % 2, H:2 * H], in1=c0sb[:, t, :], op=ALU.mult)
 
-        def p2ct(t):
+        p2s = {}
+
+        def p2t(t):
             a = acts[t // 2]
             j = t % 2
-            p2 = work.tile([P, H], F32, name="q2_%d" % t, tag="p2", bufs=2)
-            cts[("t", t)] = work.tile([P, H], F32, name="cu%d" % t, tag="ct", bufs=3)
-            nc.vector.tensor_tensor(out=p2[:], in0=a[:, j, 0:H], in1=a[:, j, 3 * H:G4], op=ALU.mult)
-            nc.vector.tensor_tensor(out=cts[("t", t)][:], in0=p1s[t][:], in1=p2[:], op=ALU.add)
+            p2s[t] = work.tile([P, H], F32, name="q2_%d" % t, tag="q2", bufs=2)
+            nc.vector.tensor_tensor(out=p2s[t][:], in0=a[:, j, 0:H], in1=a[:, j, 3 * H:G4], op=ALU.mult)
+
+        def ctt(t):
+            cts[("t", t)] = work.tile([P, H], F32, name="cu%d" % t, tag="cu", bufs=2)
+            nc.vector.tensor_tensor(out=cts[("t", t)][:], in0=p1s[t][:], in1=p2s[t][:], op=ALU.add)
             nc.sync.dma_start(out=cout[:, t, :], in_=cts[("t", t)][:])
 
         def tanh_ct(t):
-            tchs[("t", t)] = work.tile([P, H], F32, name="tu%d" % t, tag="tch", bufs=3)
+            tchs[("t", t)] = work.tile([P, H], F32, name="tu%d" % t, tag="tu", bufs=2)
             nc.scalar.activation(out=tchs[("t", t)][:], in_=cts[("t", t)][:], func=AF.Tanh)
 
         def dht(t):
-            ht = work.tile([P, H], F32, name="hu%d" % t, tag="ht", bufs=3)
+            ht = work.tile([P, H], F32, name="hu%d" % t, tag="hu", bufs=2)
             nc.vector.tensor_tensor(out=ht[:], in0=acts[t // 2][:, t % 2, 2 * H:3 * H], in1=tchs[("t", t)][:], op=ALU.mult)
             nc.sync.dma_start(out=hout[:, t, :], in_=ht[:])
 
@@ -408,18 +422,24 @@ def tile_lstmcell_t_kernel(
                     x_quant(1)
                 if k + 2 < NT // 2:
                     x_quant(k + 2)
-                if 0 <= k - HLAG < NG:
+                last = tM == NT - 1
+                if 0 <= k - HLAG < NG and not last:
                     dh(k - HLAG, nc.vector)
                 if k < NG:
                     d1(k)
-                if 1 <= k <= NG:
+                if 1 <= k <= NG and not last:
                     tanh_c(k - 1)
         tail = list(range(2 * NG, NT))
+        ct_late()
+        tanh_c(NG - 1)
         for t in tail:
             p1t(t)
-            p2ct(t)
+        for t in tail:
+            p2t(t)
+        for t in tail:
+            ctt(t)
             tanh_ct(t)
+        for k in range(NT // 2 - 1 - HLAG, NG):
+            dh(k, nc.vector)
         for t in tail:
             dht(t)
-        for k in range(NT // 2 - HLAG, NG):
-            dh(k, nc.vector)

@@ -136,12 +136,14 @@ def tile_lstmcell_t_kernel(
         load_wh(2)
         load_wh(3)
         load_w(0)
+        load_bias(nc.sync, 0)
         load_w(1)
+        load_bias(nc.sync, 1)
         x0 = load_x(0, 2)
         dma(x0[0])
-        for g in range(4):
-            load_bias(nc.sync, g)
+        load_bias(nc.sync, 2)
         load_w(2)
+        load_bias(nc.sync, 3)
         load_w(3)
         dma(x0[1])
         load_h0(4, 8)

from contextlib import ExitStack

import concourse.mybir as mybir
from concourse.masks import make_identity

F32 = mybir.dt.float32
BF16 = mybir.dt.bfloat16
U32 = mybir.dt.uint32
U8 = mybir.dt.uint8
FP8X4 = mybir.dt.float8_e4m3fn_x4
AF = mybir.ActivationFunctionType
ALU = mybir.AluOpType

B, D, H = 4096, 1024, 256
P = 128
NT = B // P
G4 = 4 * H
HALF = 512
CH = 4
NCH = NT // CH
FLOPS = 2 * B * (D + H) * G4

PIN = True
LEAD = 1
XL = 2
V_PAIRS = 1
XBUFS = 4
MFIRST = False
HLAG = 2
NBMOD = 2


def tile_lstmcell_t_kernel(
    tc, x, h0, c0,
    W_ii, b_ii, W_hi, b_hi,
    W_if, b_if, W_hf, b_hf,
    W_ig, b_ig, W_hg, b_hg,
    W_io, b_io, W_ho, b_ho,
    out_0, out_1,
):
    nc = tc.nc
    w_in = (W_ii, W_if, W_io, W_ig)
    w_rec = (W_hi, W_hf, W_ho, W_hg)
    b_in = (b_ii, b_if, b_io, b_ig)
    b_rec = (b_hi, b_hf, b_ho, b_hg)
    xv = x.rearrange("(p t) k -> p t k", t=NT)
    hv = h0.rearrange("(p t) k -> p t k", t=NT)
    cv = c0.rearrange("(p t) k -> p t k", t=NT)
    hout = out_0.rearrange("(p t) n -> p t n", t=NT)
    cout = out_1.rearrange("(p t) n -> p t n", t=NT)

    with ExitStack() as ctx:
        if PIN:
            ctx.enter_context(tc.manual_schedule())
        const = ctx.enter_context(tc.tile_pool(name="const", bufs=1))
        xin = ctx.enter_context(tc.tile_pool(name="xin", bufs=XBUFS))
        work = ctx.enter_context(tc.tile_pool(name="work", bufs=3))
        psum = ctx.enter_context(tc.psum_pool(name="psum", bufs=1))

        ident = const.tile([P, P], F32, name="ident")
        ones = const.tile([P, P], BF16, name="ones")
        brow = const.tile([P, G4], BF16, name="brow")
        bias = const.tile([P, G4], F32, name="bias")
        warm = const.tile([P, 2], F32, name="warm")
        whraw = [const.tile([P, 2, H], BF16, name="whraw%d" % g) for g in range(4)]
        whw = const.tile([P, G4], F32, name="whw")
        wraw = [const.tile([P, 2, D], BF16, name="wraw%d" % g) for g in range(4)]
        wgs = {}
        wc = const.tile([P, 2, G4], U32, name="wc", align_bytes=64)
        ws = const.tile([P, 2, G4], U8, name="ws", align_bytes=64)
        h0raw = const.tile([P, NT, H], BF16, name="h0raw")
        h0w = const.tile([P, NT, P], F32, name="h0w")
        c0sb = const.tile([P, NT, H], BF16, name="c0sb")

        xch = {}
        xts = {}
        grps = {}
        xcs = {}
        xss = {}
        ghs = {}
        gxs = {}
        tsbs = {}
        acts = {}
        cts = {}
        tchs = {}

        def load_x(c, parts=1):
            xch[c] = xin.tile([P, CH, D], BF16, name="xch%d" % c, tag="xch")
            n = CH // parts
            return [(xch[c][:, i * n:(i + 1) * n, :], xv[:, c * CH + i * n:c * CH + (i + 1) * n, :]) for i in range(parts)]

        def dma(pair):
            nc.sync.dma_start(out=pair[0], in_=pair[1])

        def load_h0(t0, t1):
            nc.sync.dma_start(out=h0raw[:, t0:t1, :], in_=hv[:, t0:t1, :])

        def load_c0(t0, t1):
            nc.sync.dma_start(out=c0sb[:, t0:t1, :], in_=cv[:, t0:t1, :])

        def load_bias(eng, g):
            eng.dma_start(out=brow[0:1, g * H:(g + 1) * H], in_=b_in[g].unsqueeze(0))
            eng.dma_start(out=brow[1:2, g * H:(g + 1) * H], in_=b_rec[g].unsqueeze(0))

        def load_wh(g):
            nc.sync.dma_start(out=whraw[g][:], in_=w_rec[g].rearrange("(j p) k -> p j k", p=P))

        def load_w(g):
            nc.sync.dma_start(out=wraw[g][:], in_=w_in[g].rearrange("(j p) k -> p j k", p=P))

        def bank(tag, name):
            return psum.tile([P, HALF], F32, name=name, tag=tag, bufs={"xt": 3, "gh": 3, "gx": 2}[tag])

        def on_scalar(t, h):
            return h == 1 and t % NBMOD != 0

        def half(h):
            return slice(h * HALF, (h + 1) * HALF)

        def tr(dst, q, src):
            nc.tensor.transpose(out=dst[:, q * P:(q + 1) * P], in_=src, identity=ident[:])

        def pairs_view(ap):
            return ap.bitcast(BF16).rearrange("p (n e) -> p n e", e=2)

        def grouped_read(pb):
            return pb[:].rearrange("p (g u r) -> p g r u", g=2, u=2)

        make_identity(nc, ident[:])
        nc.vector.memset(warm[:], 0.0)
        nc.vector.memset(brow[:], 0.0)
        nc.vector.memset(ones[:], 1.0)
        load_wh(0)
        load_wh(1)
        load_h0(0, 4)
        load_wh(2)
        load_wh(3)
        load_w(0)
        load_bias(nc.sync, 0)
        load_w(1)
        load_bias(nc.sync, 1)
        x0 = load_x(0, 2)
        dma(x0[0])
        load_bias(nc.sync, 2)
        load_w(2)
        load_bias(nc.sync, 3)
        load_w(3)
        dma(x0[1])
        load_h0(4, 8)
        dma(load_x(1)[0])
        load_c0(0, 8)
        dma(load_x(2)[0])
        load_h0(8, 16)
        dma(load_x(3)[0])
        load_c0(8, 16)
        load_h0(16, 32)
        load_c0(16, 32)
        nc.scalar.activation(out=warm[:, 1:2], in_=warm[:, 0:1], func=AF.Sigmoid)

        def wh_bank(b, tag, copy):
            pb = bank(tag, "whp%d" % b)
            for i in range(2):
                for j in range(2):
                    tr(pb, 2 * i + j, whraw[2 * b + i][:, j, :].bitcast(F32))
            copy(out=whw[:, half(b)], in_=pb[:])

        def h0_tr(c, pb):
            return [("t", pb, j, h0raw[:, c * CH + j, :].bitcast(F32)) for j in range(CH)]

        def h0_copy(c, pb, copy):
            copy(out=h0w[:, c * CH:(c + 1) * CH, :].rearrange("p t r -> p (t r)"), in_=pb[:])

        def bias_bank(h, tag, copy):
            pb = bank(tag, "bp%d" % h)
            nc.tensor.matmul(out=pb[:], lhsT=ones[:], rhs=brow[:, half(h)], start=True, stop=True)
            copy(out=bias[:, half(h)], in_=pb[:])

        def run(op):
            if op[0] == "t":
                tr(op[1], op[2], op[3])
            elif op[0] == "b":
                nc.tensor.matmul(out=ghs[(op[1], op[2])][:], lhsT=ones[:], rhs=brow[:, half(op[2])], start=False, stop=True)
            else:
                t, h, e = op[1], op[2], op[3]
                nc.tensor.matmul(
                    out=ghs[(t, h)][:],
                    lhsT=pairs_view(h0w[:, t, :])[:, :, e],
                    rhs=pairs_view(whw[:, half(h)])[:, :, e],
                    start=(e == 0),
                    stop=(e == 1 and not on_scalar(t, h)),
                )

        def weave(mm, trs):
            gaps = max(len(mm) - 1, 1)
            per = (len(trs) + gaps - 1) // gaps
            i = 0
            for n, m in enumerate(mm):
                run(m)
                if n < len(mm) - 1:
                    for op in trs[i:i + per]:
                        run(op)
                    i += per
            for op in trs[i:]:
                run(op)

        def w_tile(n, tag, copy):
            pb = bank(tag, "wp%d" % n)
            ww = wraw[n // 2][:, n % 2, :].bitcast(F32)
            for q in range(4):
                tr(pb, q, ww[:, q * P:(q + 1) * P])
            wgs[n] = work.tile([P, 2, P, 2], F32, name="wg%d" % n, tag="wg", bufs=4, align_bytes=64)
            copy(out=wgs[n][:], in_=grouped_read(pb))

        def w_quant(n):
            for g in range(2):
                nc.vector.quantize_mx(
                    out=wc[:, g, n * P:(n + 1) * P].bitcast(FP8X4),
                    scales=ws[:, g, n * P:(n + 1) * P],
                    in_=wgs[n][:, g, :, :].rearrange("p r u -> p (r u)").bitcast(BF16),
                )

        def x_copy(t):
            if t % 2 == 0:
                grps[t // 2] = work.tile([P, 2, 2, P, 2], F32, name="grp%d" % (t // 2), tag="grp", bufs=2, align_bytes=64)
            nc.scalar.copy(out=grps[t // 2][:, t % 2], in_=grouped_read(xts[t]))

        def x_quant(q):
            xcs[q] = work.tile([P, 4 * P], U32, name="xc%d" % q, tag="xc", bufs=3, align_bytes=64)
            xss[q] = work.tile([P, 4 * P], U8, name="xs%d" % q, tag="xs", bufs=3, align_bytes=64)
            nc.vector.quantize_mx(
                out=xcs[q][:].bitcast(FP8X4),
                scales=xss[q][:],
                in_=grps[q][:].rearrange("p t g r u -> p (t g r u)").bitcast(BF16),
            )

        def m_passes(t):
            for h in range(2):
                gxs[(t, h)] = bank("gx", "gx%d_%d" % (t, h))
                for g in range(2):
                    nc.tensor.matmul_mx(
                        out=gxs[(t, h)][:],
                        lhsT=xcs[t // 2][:, (2 * (t % 2) + g) * P:(2 * (t % 2) + g + 1) * P].bitcast(FP8X4),
                        lhsT_scale=xss[t // 2][:, (2 * (t % 2) + g) * P:(2 * (t % 2) + g + 1) * P],
                        rhs=wc[:, g, half(h)].bitcast(FP8X4),
                        rhs_scale=ws[:, g, half(h)],
                        start=(g == 0),
                        stop=(g == 1),
                    )

        def a_op(t, h):
            if on_scalar(t, h):
                nc.scalar.copy(out=tsbs[t][:, half(h)], in_=ghs[(t, h)][:])
                return
            nc.vector.tensor_tensor(out=tsbs[t][:, half(h)], in0=ghs[(t, h)][:], in1=bias[:, half(h)], op=ALU.add)

        def b_op(t, h):
            nc.vector.tensor_tensor(out=tsbs[t][:, half(h)], in0=gxs[(t, h)][:], in1=tsbs[t][:, half(h)], op=ALU.add)

        def c_op(t):
            if t % 2 == 0:
                acts[t // 2] = work.tile([P, 2, G4], F32, name="act%d" % (t // 2), tag="act", bufs=4)
            a = acts[t // 2]
            nc.scalar.activation(out=a[:, t % 2, 0:3 * H], in_=tsbs[t][:, 0:3 * H], func=AF.Sigmoid)
            nc.scalar.activation(out=a[:, t % 2, 3 * H:G4], in_=tsbs[t][:, 3 * H:G4], func=AF.Tanh)

        def d_eng(k):
            return nc.vector if k >= NT // 2 - V_PAIRS else nc.gpsimd

        def d1(k):
            eng = d_eng(k)
            a = acts[k]
            p1 = work.tile([P, 2, H], F32, name="p1_%d" % k, tag="p1", bufs=2)
            p2 = work.tile([P, 2, H], F32, name="p2_%d" % k, tag="p2", bufs=2)
            cts[k] = work.tile([P, 2, H], F32, name="ct%d" % k, tag="ct", bufs=3)
            eng.tensor_tensor(out=p1[:], in0=a[:, :, H:2 * H], in1=c0sb[:, 2 * k:2 * k + 2, :], op=ALU.mult)
            eng.tensor_tensor(out=p2[:], in0=a[:, :, 0:H], in1=a[:, :, 3 * H:G4], op=ALU.mult)
            if k == NG - 1:
                late_ct.append((k, p1, p2))
                return
            eng.tensor_tensor(out=cts[k][:], in0=p1[:], in1=p2[:], op=ALU.add)
            nc.sync.dma_start(out=cout[:, 2 * k:2 * k + 2, :], in_=cts[k][:])

        late_ct = []

        def ct_late():
            k, p1, p2 = late_ct[0]
            nc.vector.tensor_tensor(out=cts[k][:], in0=p1[:], in1=p2[:], op=ALU.add)
            nc.sync.dma_start(out=cout[:, 2 * k:2 * k + 2, :], in_=cts[k][:])

        def tanh_c(k):
            tchs[k] = work.tile([P, 2, H], F32, name="tch%d" % k, tag="tch", bufs=3)
            nc.scalar.activation(out=tchs[k][:], in_=cts[k][:], func=AF.Tanh)

        def dh(k, eng=None):
            ht = work.tile([P, 2, H], F32, name="ht%d" % k, tag="ht", bufs=3)
            (eng or d_eng(k)).tensor_tensor(out=ht[:], in0=acts[k][:, :, 2 * H:3 * H], in1=tchs[k][:], op=ALU.mult)
            nc.sync.dma_start(out=hout[:, 2 * k:2 * k + 2, :], in_=ht[:])

        p1s = {}

        def c_half(t, h):
            if t % 2 == 0 and h == 0:
                acts[t // 2] = work.tile([P, 2, G4], F32, name="act%d" % (t // 2), tag="act", bufs=4)
            a = acts[t // 2]
            j = t % 2
            if h == 0:
                nc.scalar.activation(out=a[:, j, 0:2 * H], in_=tsbs[t][:, 0:2 * H], func=AF.Sigmoid)
            else:
                nc.scalar.activation(out=a[:, j, 3 * H:G4], in_=tsbs[t][:, 3 * H:G4], func=AF.Tanh)
                nc.scalar.activation(out=a[:, j, 2 * H:3 * H], in_=tsbs[t][:, 2 * H:3 * H], func=AF.Sigmoid)

        def p1t(t):
            p1s[t] = work.tile([P, H], F32, name="q1_%d" % t, tag="q1", bufs=2)
            nc.vector.tensor_tensor(out=p1s[t][:], in0=acts[t // 2][:, t % 2, H:2 * H], in1=c0sb[:, t, :], op=ALU.mult)

        p2s = {}

        def p2t(t):
            a = acts[t // 2]
            j = t % 2
            p2s[t] = work.tile([P, H], F32, name="q2_%d" % t, tag="q2", bufs=2)
            nc.vector.tensor_tensor(out=p2s[t][:], in0=a[:, j, 0:H], in1=a[:, j, 3 * H:G4], op=ALU.mult)

        def ctt(t):
            cts[("t", t)] = work.tile([P, H], F32, name="cu%d" % t, tag="cu", bufs=2)
            nc.vector.tensor_tensor(out=cts[("t", t)][:], in0=p1s[t][:], in1=p2s[t][:], op=ALU.add)
            nc.sync.dma_start(out=cout[:, t, :], in_=cts[("t", t)][:])

        def tanh_ct(t):
            tchs[("t", t)] = work.tile([P, H], F32, name="tu%d" % t, tag="tu", bufs=2)
            nc.scalar.activation(out=tchs[("t", t)][:], in_=cts[("t", t)][:], func=AF.Tanh)

        def dht(t):
            ht = work.tile([P, H], F32, name="hu%d" % t, tag="hu", bufs=2)
            nc.vector.tensor_tensor(out=ht[:], in0=acts[t // 2][:, t % 2, 2 * H:3 * H], in1=tchs[("t", t)][:], op=ALU.mult)
            nc.sync.dma_start(out=hout[:, t, :], in_=ht[:])

        def x_stage(t):
            xts[t] = bank("xt", "xt%d" % t)
            xw = xch[t // CH][:, t % CH, :].bitcast(F32)
            return [("t", xts[t], q, xw[:, q * P:(q + 1) * P]) for q in range(4)]

        def x_done(t):
            x_copy(t)
            if t % CH == CH - 1 and t // CH + XBUFS < NCH:
                dma(load_x(t // CH + XBUFS)[0])

        def h_stage(s):
            tsbs[s] = work.tile([P, G4], F32, name="tsb%d" % s, tag="tsb", bufs=LEAD + 3)
            for h in range(2):
                ghs[(s, h)] = bank("gh", "gh%d_%d" % (s, h))
            mm = [("m", s, h, e) for h in range(2) for e in range(2)]
            if on_scalar(s, 1):
                mm = mm + [("b", s, 1)]
            return mm

        vcopy = nc.vector.tensor_copy
        scopy = nc.scalar.copy
        wh_bank(0, "xt", vcopy)
        pb0 = bank("xt", "h0p0")
        weave([], h0_tr(0, pb0))
        h0_copy(0, pb0, scopy)
        wh_bank(1, "gx", vcopy)
        for s in range(LEAD):
            weave(h_stage(s), [])
        for n in range(4):
            w_tile(n, "gx" if n % 2 == 0 else "xt", scopy if n % 2 == 0 else vcopy)
        for n in range(4):
            w_quant(n)
        for t in range(XL):
            weave([], x_stage(t))
            x_done(t)
        bias_bank(0, "gx", vcopy)
        bias_bank(1, "gx", scopy)
        for s in range(LEAD):
            a_op(s, 0)
            a_op(s, 1)
        for n in range(4, 8):
            w_tile(n, "gx" if n % 2 == 0 else "xt", scopy if n % 2 == 0 else vcopy)
        x_quant(0)
        for n in range(4, 8):
            w_quant(n)

        NG = NT // 2 - V_PAIRS
        for s in range(LEAD, NT + LEAD):
            tM = s - LEAD
            if tM < 2:
                x_now = [2 * tM + 2, 2 * tM + 3]
            else:
                x_now = [tM + 4]
            x_now = [t for t in x_now if t < NT]
            mm = []
            trs = []
            hc = None
            if s < NT:
                mm = h_stage(s)
            for t in x_now:
                trs = trs + x_stage(t)
            if s % CH == 2 and s + 2 < NT:
                hc = (s + 2) // CH
                hpb = bank("xt", "h0p%d" % hc)
                trs = trs + h0_tr(hc, hpb)
            weave(mm, trs)
            m_passes(tM)
            for t in x_now:
                x_done(t)
            if hc is not None:
                h0_copy(hc, hpb, scopy)
            if s < NT:
                a_op(s, 0)
                a_op(s, 1)
            if tM < 2 * NG:
                b_op(tM, 0)
                b_op(tM, 1)
                c_op(tM)
            else:
                b_op(tM, 0)
                c_half(tM, 0)
                b_op(tM, 1)
                c_half(tM, 1)
            if tM % 2 == 1:
                k = tM // 2
                if k == 0:
                    x_quant(1)
                if k + 2 < NT // 2:
                    x_quant(k + 2)
                last = tM == NT - 1
                if 0 <= k - HLAG < NG and not last:
                    dh(k - HLAG, nc.vector)
                if k < NG:
                    d1(k)
                if 1 <= k <= NG and not last:
                    tanh_c(k - 1)
        tail = list(range(2 * NG, NT))
        ct_late()
        tanh_c(NG - 1)
        for t in tail:
            p1t(t)
        for t in tail:
            p2t(t)
        for t in tail:
            ctt(t)
            tanh_ct(t)
        for k in range(NT // 2 - 1 - HLAG, NG):
            dh(k, nc.vector)
        for t in tail:
            dht(t)
